import numpy as np
import ml_dtypes


def mxq(x, axis, fmt="e4m3"):
    dtype, down = {"e4m3": (ml_dtypes.float8_e4m3fn, 7), "e5m2": (ml_dtypes.float8_e5m2, 14)}[fmt]
    v = np.moveaxis(np.asarray(x, np.float32).astype(ml_dtypes.bfloat16).astype(np.float64), axis, -1)
    blocks = v.reshape(v.shape[:-1] + (-1, 32))
    amax = np.abs(blocks).max(-1, keepdims=True)
    byte = np.maximum(np.where(amax > 0, np.frexp(amax)[1] - 1 + 127, 0) - down, 1)
    scale = np.exp2(byte - 127.0)
    codes = (blocks / scale).astype(np.float32).astype(dtype).astype(np.float64)
    return np.moveaxis((codes * scale).reshape(v.shape), -1, axis)


WIDE = False


def mx_kscale(k):
    if not WIDE:
        return np.ones(k)
    levels = np.array([10, -10, 5, -5, 0])
    a = np.random.permutation(np.resize(levels, k // 512 * 4)).reshape(k // 512, 4)
    idx = np.arange(k)
    return np.exp2(a[idx // 512, idx % 128 // 32])


BF16 = ml_dtypes.bfloat16


def bf(x):
    return np.asarray(x, np.float32).astype(BF16)


def f64(x):
    return np.asarray(x).astype(np.float64)


B, O, I, LQ, LS, D = 256, 2, 16, 32, 32, 16
FS = LS * D
KV = I * LS
EPS = 1e-5
SHIFT = 14.0


def setup_inputs():
    s = mx_kscale(FS)
    enc = np.random.standard_normal((B, I, FS)) * s
    return {
        "scores": bf(-SHIFT + 1.5 * np.random.standard_normal((B, O, I, LQ, LS))),
        "final_encoder_out": bf(enc.reshape(B, I * LS, D)),
        "WV_w": bf(np.random.standard_normal((O, FS, FS)) * 1.5 / np.sqrt(FS) / s),
        "WV_b": bf(np.random.standard_normal((O, FS)) * 0.2),
    }


def reference(scores, final_encoder_out, WV_w, WV_b):
    encq = mxq(f64(final_encoder_out).reshape(B * I, FS), 1, "e4m3")
    wq = mxq(f64(WV_w).reshape(O * FS, FS), 1, "e4m3")
    v = (encq @ wq.T) + f64(WV_b).reshape(O * FS)
    v = np.swapaxes(v.reshape(B, I, O, LS, D), 1, 2).reshape(B, O, KV, D)
    e = np.exp(f64(scores))
    attn = e / (e.sum(-1, keepdims=True) + EPS)
    attn = np.swapaxes(attn, 2, 3).reshape(B, O, LQ, KV)
    z = mxq(attn, 3, "e4m3") @ mxq(v, 2, "e4m3")
    coeff = 1.0 / np.sqrt(D)
    return (coeff * z).reshape(B, O * LQ, D)

@@ -1,0 +1,308 @@
+from contextlib import ExitStack
+
+import concourse.mybir as mybir
+from concourse.masks import make_identity
+
+F32 = mybir.dt.float32
+BF16 = mybir.dt.bfloat16
+U32 = mybir.dt.uint32
+U8 = mybir.dt.uint8
+I32 = mybir.dt.int32
+FP8X4 = mybir.dt.float8_e4m3fn_x4
+ACT = mybir.ActivationFunctionType
+ALU = mybir.AluOpType
+
+P = 128
+PACK = 4
+B, O, I, LQ, LS, D = 256, 2, 16, 32, 32, 16
+FS = LS * D
+EPS = 1e-5
+IH = I // PACK
+IL = PACK
+FLOPS = 2 * (B * I) * FS * (O * FS) + 2 * (B * O) * LQ * (I * LS) * D
+
+ROW = IL * LQ * LS
+TILES = B * O * IH // P
+TILE_B = P // (O * IH)
+HALF_Q = LQ // 2
+BANK_Q = 8
+
+QUARTERS = 4
+QUARTER_B = B // QUARTERS
+QUARTER_COLS = QUARTER_B * IH
+QUARTER_TILES = TILES // QUARTERS
+ENC_CHUNKS = B * IH // P
+GROUP_B = 4
+ZERO_COLS = P - LS
+
+PAIRS_PER_TILE = 6
+
+
+def tile_localcrossattention_pa_t_kernel(tc, scores, final_encoder_out, WV_w, WV_b, out):
+    nc = tc.nc
+
+    score_rows = scores.rearrange("b o (h l) q k -> (b o h) (l q k)", h=IH)
+    enc_rows = final_encoder_out.rearrange("b (h l s) d -> (b h) (l s d)", h=IH, l=IL)
+    w_rows = WV_w.rearrange("o (c p) f -> p (o c) f", p=P)
+    out_view = out.rearrange("(n j) (o q) d -> j o q n d", j=GROUP_B, o=O)
+
+    with ExitStack() as stack:
+        const = stack.enter_context(tc.tile_pool(name="const", bufs=1))
+        x_pool = stack.enter_context(tc.tile_pool(name="x", bufs=3))
+        e_pool = stack.enter_context(tc.tile_pool(name="e", bufs=3))
+        sum_pool = stack.enter_context(tc.tile_pool(name="sums", bufs=4))
+        attn_pool = stack.enter_context(tc.tile_pool(name="attn", bufs=2))
+        a_stage = stack.enter_context(tc.tile_pool(name="a_stage", bufs=2))
+        a_keep = stack.enter_context(tc.tile_pool(name="a_keep", bufs=5))
+        enc_stage = stack.enter_context(tc.tile_pool(name="enc_stage", bufs=2))
+        res_pool = stack.enter_context(tc.tile_pool(name="res", bufs=2))
+        ps_words = stack.enter_context(tc.psum_pool(name="ps_words", bufs=1))
+        ps_attn = stack.enter_context(tc.psum_pool(name="ps_attn", bufs=3))
+        ps_v = stack.enter_context(tc.psum_pool(name="ps_v", bufs=2))
+        ps_out = stack.enter_context(tc.psum_pool(name="ps_out", bufs=2))
+
+        ident_bf = const.tile([P, P], BF16)
+        make_identity(nc, ident_bf[:])
+        ident_f32 = const.tile([P, P], F32)
+        make_identity(nc, ident_f32[:])
+
+        x_tiles = {}
+
+        def load_scores(g):
+            x = x_pool.tile([P, ROW], BF16, name="x", tag="x")
+            nc.sync.dma_start(out=x[:], in_=score_rows[g * P : (g + 1) * P, :])
+            x_tiles[g] = x
+
+        load_scores(0)
+
+        bias_bf = const.tile([P, O * D], BF16)
+        for il in range(IL):
+            nc.sync.dma_start(
+                out=bias_bf[il * LS : (il + 1) * LS, :].rearrange("k (o d) -> k o d", o=O),
+                in_=WV_b.rearrange("o (k d) -> k o d", d=D),
+            )
+        bias_col = const.tile([P, O * D], F32)
+        nc.vector.tensor_copy(out=bias_col[:], in_=bias_bf[:])
+
+        z_codes = const.tile([P, O * D * P + ZERO_COLS], U32, align_bytes=64)
+        nc.vector.memset(z_codes[:].bitcast(I32), 0)
+        z_scales = const.tile([P, O * D * P], U8, align_bytes=64)
+
+        with tc.tile_pool(name="w_prep", bufs=1) as w_prep:
+            w_nat = w_prep.tile([P, O * FS // P, FS], BF16)
+            nc.sync.dma_start(out=w_nat[:], in_=w_rows)
+            w_grp = w_prep.tile([P, O * FS * PACK], BF16, align_bytes=64)
+            w_grp_words = w_grp[:].bitcast(F32).rearrange("p (o d k u) -> p o d k u", o=O, d=D, k=LS)
+            k_rows = P // D
+            for pair in range(O * FS // P // 2):
+                wt = ps_words.tile([P, 2, 2, P], F32, name="wt", tag="words")
+                for ci in range(2):
+                    w_words = w_nat[:, 2 * pair + ci, :].bitcast(F32)
+                    for u in range(2):
+                        nc.tensor.transpose(
+                            out=wt[:, ci, u, :], in_=w_words[:, u * P : (u + 1) * P], identity=ident_f32[:]
+                        )
+                for ci in range(2):
+                    o, kc = divmod(2 * pair + ci, LS // k_rows)
+                    nc.vector.tensor_copy(
+                        out=w_grp_words[:, o, :, kc * k_rows : (kc + 1) * k_rows, :],
+                        in_=wt[:, ci].rearrange("p u (k d) -> p d k u", d=D),
+                    )
+            w_codes = w_prep.tile([P, O * FS], U32, align_bytes=64)
+            w_scales = w_prep.tile([P, O * FS], U8, align_bytes=64)
+            nc.vector.memset(w_scales[:].bitcast(I32), 0)
+            nc.vector.quantize_mx(out=w_codes[:].bitcast(FP8X4), scales=w_scales[:], in_=w_grp[:])
+            nc.vector.tensor_copy(
+                out=z_codes[:, 0 : O * D * P].bitcast(I32).rearrange("p (g c) -> p g c", c=P)[:, :, ZERO_COLS:P],
+                in_=w_codes[:].bitcast(I32).rearrange("p (g k) -> p g k", k=LS),
+            )
+            z_scale_words = z_scales[:].bitcast(I32).rearrange("p (g r w) -> p g r w", r=IL, w=LS // 4)
+            for il in range(IL):
+                nc.vector.tensor_copy(
+                    out=z_scale_words[:, :, il, :],
+                    in_=w_scales[:].bitcast(I32).rearrange("p (g w) -> p g w", w=LS // 4),
+                )
+
+        v_stage = stack.enter_context(tc.tile_pool(name="v_stage", bufs=2))
+        v_keep = stack.enter_context(tc.tile_pool(name="v_keep", bufs=6))
+
+        enc_codes = const.tile([P, IL, B * IH], U32, align_bytes=64)
+        enc_scales = const.tile([P, IL, B * IH], U8, align_bytes=64)
+
+        def prepare_enc(c):
+            e_nat = enc_stage.tile([P, IL * FS], BF16)
+            nc.sync.dma_start(out=e_nat[:], in_=enc_rows[c * P : (c + 1) * P, :])
+            e_words = e_nat[:].bitcast(F32)
+            e_grp = enc_stage.tile([P, IL * P * PACK], BF16, align_bytes=64)
+            e_grp_words = e_grp[:].bitcast(F32).rearrange("p (l m u) -> p l m u", l=IL, u=2)
+            for pair in range(IL // 2):
+                et = ps_words.tile([P, 2, 2, P], F32, name="et", tag="words")
+                for li in range(2):
+                    for u in range(2):
+                        first = ((2 * pair + li) * 2 + u) * P
+                        nc.tensor.transpose(
+                            out=et[:, li, u, :], in_=e_words[:, first : first + P], identity=ident_f32[:]
+                        )
+                nc.vector.tensor_copy(
+                    out=e_grp_words[:, 2 * pair : 2 * pair + 2, :, :],
+                    in_=et[:].rearrange("p l u m -> p l m u"),
+                )
+            cols = slice(c * P, (c + 1) * P)
+            for il in range(IL):
+                nc.vector.quantize_mx(
+                    out=enc_codes[:, il, cols].bitcast(FP8X4),
+                    scales=enc_scales[:, il, cols],
+                    in_=e_grp[:, il * P * PACK : (il + 1) * P * PACK],
+                )
+
+        prepare_enc(0)
+        prepare_enc(1)
+        load_scores(1)
+
+        attn_tiles = {}
+
+        def softmax(g):
+            x_by_query = x_tiles[g][:].rearrange("p (l q k) -> p q l k", l=IL, q=LQ)
+            attn = attn_pool.tile([P, ROW], BF16)
+            for half in range(LQ // HALF_Q):
+                groups = HALF_Q * IL
+                e = e_pool.tile([P, groups * LS], F32)
+                nc.scalar.activation(
+                    out=e[:].rearrange("p (q l k) -> p q l k", l=IL, k=LS),
+                    in_=x_by_query[:, half * HALF_Q : (half + 1) * HALF_Q],
+                    func=ACT.Exp,
+                )
+                e_groups = e[:].rearrange("p (g k) -> p g k", k=LS)
+                sums = sum_pool.tile([P, groups], F32)
+                nc.vector.tensor_reduce(out=sums[:], in_=e_groups, axis=mybir.AxisListType.X, op=ALU.add)
+                denom = sum_pool.tile([P, groups], F32)
+                nc.vector.tensor_scalar_add(out=denom[:], in0=sums[:], scalar1=EPS)
+                recip = sum_pool.tile([P, groups], F32)
+                nc.vector.reciprocal(out=recip[:], in_=denom[:])
+                nc.vector.tensor_tensor(
+                    out=attn[:, half * groups * LS : (half + 1) * groups * LS].rearrange("p (g k) -> p g k", k=LS),
+                    in0=e_groups,
+                    in1=recip[:].unsqueeze(2).to_broadcast([P, groups, LS]),
+                    op=ALU.mult,
+                )
+            attn_tiles[g] = attn
+
+        attn_q = {}
+
+        def transpose_and_quantise(g):
+            attn = attn_tiles[g]
+            a_grp = a_stage.tile([P, ROW], BF16, align_bytes=64)
+            a_grp_banks = a_grp[:].rearrange("p (c n x) -> p c n x", n=LQ // BANK_Q, x=BANK_Q * PACK)
+            for bank in range(LQ // BANK_Q):
+                at = ps_attn.tile([P, O * TILE_B * BANK_Q * PACK], BF16)
+                at_by_query = at[:].rearrange("p (o b q t) -> p b o q t", o=O, b=TILE_B, q=BANK_Q)
+                for qi in range(BANK_Q):
+                    q = bank * BANK_Q + qi
+                    nc.tensor.transpose(
+                        out=at_by_query[:, :, :, qi, :], in_=attn[:, q * P : (q + 1) * P], identity=ident_bf[:]
+                    )
+                nc.scalar.copy(
+                    out=a_grp_banks[:, :, bank, :],
+                    in_=at[:].rearrange("p (c x) -> p c x", x=BANK_Q * PACK),
+                )
+            a_codes = a_keep.tile([P, ROW // PACK], U32, name="a_codes", tag="a_codes", align_bytes=64)
+            a_scales = a_keep.tile([P, ROW // PACK], U8, name="a_scales", tag="a_scales", align_bytes=64)
+            nc.vector.quantize_mx(out=a_codes[:].bitcast(FP8X4), scales=a_scales[:], in_=a_grp[:])
+            attn_q[g] = (a_codes, a_scales)
+
+        v_q = {}
+        v_grps = {}
+        v_cols = QUARTER_B // GROUP_B * D * GROUP_B
+
+        def project_pair(quarter, o, d_pair):
+            if d_pair == 0:
+                v_grps[(quarter, o)] = v_stage.tile(
+                    [P, v_cols * PACK], BF16, name="v_grp", tag="v_grp", align_bytes=64
+                )
+            v_grp = v_grps[(quarter, o)]
+            v_grp_by_d = v_grp[:].rearrange("p (n d x) -> p n d x", d=D, x=GROUP_B * PACK)
+            cols = slice(quarter * QUARTER_COLS, (quarter + 1) * QUARTER_COLS)
+            acc = ps_v.tile([P, 2, QUARTER_COLS], F32)
+            for di in range(2):
+                od = o * D + 2 * d_pair + di
+                for il in range(IL):
+                    first = od * P + ZERO_COLS - il * LS
+                    nc.tensor.matmul_mx(
+                        out=acc[:, di, :],
+                        lhsT=z_codes[:, first : first + P].bitcast(FP8X4),
+                        lhsT_scale=z_scales[:, od * P : (od + 1) * P],
+                        rhs=enc_codes[:, il, cols].bitcast(FP8X4),
+                        rhs_scale=enc_scales[:, il, cols],
+                        start=(il == 0),
+                        stop=(il == IL - 1),
+                    )
+            for di in range(2):
+                d = 2 * d_pair + di
+                nc.scalar.activation(
+                    out=v_grp_by_d[:, :, d, :],
+                    in_=acc[:, di, :].rearrange("p (n x) -> p n x", x=GROUP_B * PACK),
+                    func=ACT.Identity,
+                    bias=bias_col[:, o * D + d : o * D + d + 1],
+                )
+            if d_pair == D // 2 - 1:
+                v_codes = v_keep.tile([P, v_cols], U32, name="v_codes", tag="v_codes", align_bytes=64)
+                v_scales = v_keep.tile([P, v_cols], U8, name="v_scales", tag="v_scales", align_bytes=64)
+                nc.vector.quantize_mx(out=v_codes[:].bitcast(FP8X4), scales=v_scales[:], in_=v_grp[:])
+                v_q[(quarter, o)] = (v_codes, v_scales)
+
+        res_tiles = {}
+        pass_cols = D * GROUP_B
+
+        def attend(g):
+            quarter, gi = divmod(g, QUARTER_TILES)
+            groups = TILE_B // GROUP_B
+            a_codes, a_scales = attn_q[g]
+            o_acc = ps_out.tile([P, O, groups, D, GROUP_B], F32)
+            for o in range(O):
+                v_codes, v_scales = v_q[(quarter, o)]
+                for s in range(groups):
+                    a_cols = slice((o * groups + s) * P, (o * groups + s + 1) * P)
+                    v_first = (gi * groups + s) * pass_cols
+                    nc.tensor.matmul_mx(
+                        out=o_acc[:, o, s].rearrange("p d j -> p (d j)"),
+                        lhsT=a_codes[:, a_cols].bitcast(FP8X4),
+                        lhsT_scale=a_scales[:, a_cols],
+                        rhs=v_codes[:, v_first : v_first + pass_cols].bitcast(FP8X4),
+                        rhs_scale=v_scales[:, v_first : v_first + pass_cols],
+                        start=True,
+                        stop=True,
+                    )
+            if gi == 0:
+                res_tiles[quarter] = res_pool.tile(
+                    [P, O, QUARTER_TILES, groups, D], F32, name="res", tag="res"
+                )
+            res = res_tiles[quarter]
+            for j in range(GROUP_B):
+                rows = slice(j * LQ, (j + 1) * LQ)
+                nc.scalar.mul(out=res[rows, :, gi, :, :], in_=o_acc[rows, :, :, :, j], mul=1.0 / 4.0)
+            if gi == QUARTER_TILES - 1:
+                n_groups = QUARTER_TILES * groups
+                for j in range(GROUP_B):
+                    for o in range(O):
+                        nc.sync.dma_start(
+                            out=out_view[j, o, :, quarter * n_groups : (quarter + 1) * n_groups, :],
+                            in_=res[j * LQ : (j + 1) * LQ, o].rearrange("q g s d -> q (g s) d"),
+                        )
+
+        pairs = [(quarter, o, d_pair) for quarter in range(QUARTERS) for o in range(O) for d_pair in range(D // 2)]
+        pairs_of_a_quarter = O * D // 2
+        pairs_done = 0
+        attended = 0
+        for g in range(TILES):
+            if g + 2 < TILES:
+                load_scores(g + 2)
+            softmax(g)
+            transpose_and_quantise(g)
+            if g + 2 < ENC_CHUNKS:
+                prepare_enc(g + 2)
+            for quarter, o, d_pair in pairs[pairs_done : pairs_done + PAIRS_PER_TILE]:
+                project_pair(quarter, o, d_pair)
+            pairs_done = min(pairs_done + PAIRS_PER_TILE, len(pairs))
+            while attended <= g and attended // QUARTER_TILES < pairs_done // pairs_of_a_quarter:
+                attend(attended)
+                attended += 1

@@ -26,6 +26,7 @@ TILES = B * O * IH // P
 TILE_B = P // (O * IH)
 HALF_Q = LQ // 2
 BANK_Q = 8
+GPSIMD_GROUPS = 32
 
 QUARTERS = 4
 QUARTER_B = B // QUARTERS
@@ -179,10 +180,20 @@ def tile_localcrossattention_pa_t_kernel(tc, scores, final_encoder_out, WV_w, WV
                 nc.vector.tensor_scalar_add(out=denom[:], in0=sums[:], scalar1=EPS)
                 recip = sum_pool.tile([P, groups], F32)
                 nc.vector.reciprocal(out=recip[:], in_=denom[:])
+                attn_groups = attn[:, half * groups * LS : (half + 1) * groups * LS].rearrange(
+                    "p (g k) -> p g k", k=LS
+                )
+                split = groups - GPSIMD_GROUPS
                 nc.vector.tensor_tensor(
-                    out=attn[:, half * groups * LS : (half + 1) * groups * LS].rearrange("p (g k) -> p g k", k=LS),
-                    in0=e_groups,
-                    in1=recip[:].unsqueeze(2).to_broadcast([P, groups, LS]),
+                    out=attn_groups[:, 0:split, :],
+                    in0=e_groups[:, 0:split, :],
+                    in1=recip[:, 0:split].unsqueeze(2).to_broadcast([P, split, LS]),
+                    op=ALU.mult,
+                )
+                nc.gpsimd.tensor_tensor(
+                    out=attn_groups[:, split:groups, :],
+                    in0=e_groups[:, split:groups, :],
+                    in1=recip[:, split:groups].unsqueeze(2).to_broadcast([P, GPSIMD_GROUPS, LS]),
                     op=ALU.mult,
                 )
             attn_tiles[g] = attn

@@ -24,9 +24,12 @@ FLOPS = 2 * (B * I) * FS * (O * FS) + 2 * (B * O) * LQ * (I * LS) * D
 ROW = IL * LQ * LS
 TILES = B * O * IH // P
 TILE_B = P // (O * IH)
+HALVES = 2 * TILES
 HALF_Q = LQ // 2
+GROUPS = HALF_Q * IL
+HALF = GROUPS * LS
 BANK_Q = 8
-GPSIMD_GROUPS = 32
+HALF_BANKS = HALF_Q // BANK_Q
 
 QUARTERS = 4
 QUARTER_B = B // QUARTERS
@@ -34,9 +37,13 @@ QUARTER_COLS = QUARTER_B * IH
 QUARTER_TILES = TILES // QUARTERS
 ENC_CHUNKS = B * IH // P
 GROUP_B = 4
+TILE_GROUPS = TILE_B // GROUP_B
+PASS_COLS = D * GROUP_B
+V_COLS = QUARTER_B * D
 ZERO_COLS = P - LS
+D_PAIRS = D // 2
 
-PAIRS_PER_TILE = 6
+PAIRS_PER_STEP = 2
 
 
 def tile_localcrossattention_pa_t_kernel(tc, scores, final_encoder_out, WV_w, WV_b, out):
@@ -48,17 +55,12 @@ def tile_localcrossattention_pa_t_kernel(tc, scores, final_encoder_out, WV_w, WV
     out_view = out.rearrange("(n j) (o q) d -> j o q n d", j=GROUP_B, o=O)
 
     with ExitStack() as stack:
+        stack.enter_context(tc.manual_schedule())
         const = stack.enter_context(tc.tile_pool(name="const", bufs=1))
         x_pool = stack.enter_context(tc.tile_pool(name="x", bufs=3))
-        e_pool = stack.enter_context(tc.tile_pool(name="e", bufs=3))
+        e_pool = stack.enter_context(tc.tile_pool(name="e", bufs=5))
         sum_pool = stack.enter_context(tc.tile_pool(name="sums", bufs=4))
-        attn_pool = stack.enter_context(tc.tile_pool(name="attn", bufs=2))
-        a_stage = stack.enter_context(tc.tile_pool(name="a_stage", bufs=2))
-        a_keep = stack.enter_context(tc.tile_pool(name="a_keep", bufs=5))
-        enc_stage = stack.enter_context(tc.tile_pool(name="enc_stage", bufs=2))
-        res_pool = stack.enter_context(tc.tile_pool(name="res", bufs=2))
-        ps_words = stack.enter_context(tc.psum_pool(name="ps_words", bufs=1))
-        ps_attn = stack.enter_context(tc.psum_pool(name="ps_attn", bufs=3))
+        ps_t = stack.enter_context(tc.psum_pool(name="ps_t", bufs=4))
         ps_v = stack.enter_context(tc.psum_pool(name="ps_v", bufs=2))
         ps_out = stack.enter_context(tc.psum_pool(name="ps_out", bufs=2))
 
@@ -68,13 +70,27 @@ def tile_localcrossattention_pa_t_kernel(tc, scores, final_encoder_out, WV_w, WV
         make_identity(nc, ident_f32[:])
 
         x_tiles = {}
+        e_tiles = {}
 
         def load_scores(g):
             x = x_pool.tile([P, ROW], BF16, name="x", tag="x")
             nc.sync.dma_start(out=x[:], in_=score_rows[g * P : (g + 1) * P, :])
             x_tiles[g] = x
 
+        def exp(h):
+            g, half = divmod(h, 2)
+            x_by_query = x_tiles[g][:].rearrange("p (l q k) -> p q l k", l=IL, q=LQ)
+            e = e_pool.tile([P, HALF], F32, name="e", tag="e")
+            nc.scalar.activation(
+                out=e[:].rearrange("p (q l k) -> p q l k", l=IL, k=LS),
+                in_=x_by_query[:, half * HALF_Q : (half + 1) * HALF_Q],
+                func=ACT.Exp,
+            )
+            e_tiles[h] = e
+
         load_scores(0)
+        exp(0)
+        exp(1)
 
         bias_bf = const.tile([P, O * D], BF16)
         for il in range(IL):
@@ -83,20 +99,24 @@ def tile_localcrossattention_pa_t_kernel(tc, scores, final_encoder_out, WV_w, WV
                 in_=WV_b.rearrange("o (k d) -> k o d", d=D),
             )
         bias_col = const.tile([P, O * D], F32)
-        nc.vector.tensor_copy(out=bias_col[:], in_=bias_bf[:])
 
         z_codes = const.tile([P, O * D * P + ZERO_COLS], U32, align_bytes=64)
         nc.vector.memset(z_codes[:].bitcast(I32), 0)
         z_scales = const.tile([P, O * D * P], U8, align_bytes=64)
+        enc_codes = const.tile([P, IL, B * IH], U32, align_bytes=64)
+        enc_scales = const.tile([P, IL, B * IH], U8, align_bytes=64)
 
-        with tc.tile_pool(name="w_prep", bufs=1) as w_prep:
+        with tc.tile_pool(name="w_prep", bufs=1) as w_prep, tc.tile_pool(name="enc_stage", bufs=2) as enc_stage:
             w_nat = w_prep.tile([P, O * FS // P, FS], BF16)
             nc.sync.dma_start(out=w_nat[:], in_=w_rows)
+            w_scales = w_prep.tile([P, O * FS], U8, align_bytes=64)
+            nc.vector.memset(w_scales[:].bitcast(I32), 0)
+            nc.vector.tensor_copy(out=bias_col[:], in_=bias_bf[:])
             w_grp = w_prep.tile([P, O * FS * PACK], BF16, align_bytes=64)
             w_grp_words = w_grp[:].bitcast(F32).rearrange("p (o d k u) -> p o d k u", o=O, d=D, k=LS)
             k_rows = P // D
             for pair in range(O * FS // P // 2):
-                wt = ps_words.tile([P, 2, 2, P], F32, name="wt", tag="words")
+                wt = ps_t.tile([P, 2, 2, P], F32, name="wt", tag="t")
                 for ci in range(2):
                     w_words = w_nat[:, 2 * pair + ci, :].bitcast(F32)
                     for u in range(2):
@@ -105,14 +125,38 @@ def tile_localcrossattention_pa_t_kernel(tc, scores, final_encoder_out, WV_w, WV
                         )
                 for ci in range(2):
                     o, kc = divmod(2 * pair + ci, LS // k_rows)
-                    nc.vector.tensor_copy(
+                    nc.scalar.copy(
                         out=w_grp_words[:, o, :, kc * k_rows : (kc + 1) * k_rows, :],
                         in_=wt[:, ci].rearrange("p u (k d) -> p d k u", d=D),
                     )
             w_codes = w_prep.tile([P, O * FS], U32, align_bytes=64)
-            w_scales = w_prep.tile([P, O * FS], U8, align_bytes=64)
-            nc.vector.memset(w_scales[:].bitcast(I32), 0)
             nc.vector.quantize_mx(out=w_codes[:].bitcast(FP8X4), scales=w_scales[:], in_=w_grp[:])
+
+            for c in range(ENC_CHUNKS):
+                e_nat = enc_stage.tile([P, IL * FS], BF16, bufs=4)
+                nc.sync.dma_start(out=e_nat[:], in_=enc_rows[c * P : (c + 1) * P, :])
+                e_words = e_nat[:].bitcast(F32)
+                e_grp = enc_stage.tile([P, IL * P * PACK], BF16, align_bytes=64)
+                e_grp_words = e_grp[:].bitcast(F32).rearrange("p (l m u) -> p l m u", l=IL, u=2)
+                for pair in range(IL // 2):
+                    et = ps_t.tile([P, 2, 2, P], F32, name="et", tag="t")
+                    for li in range(2):
+                        for u in range(2):
+                            first = ((2 * pair + li) * 2 + u) * P
+                            nc.tensor.transpose(
+                                out=et[:, li, u, :], in_=e_words[:, first : first + P], identity=ident_f32[:]
+                            )
+                    nc.scalar.copy(
+                        out=e_grp_words[:, 2 * pair : 2 * pair + 2, :, :],
+                        in_=et[:].rearrange("p l u m -> p l m u"),
+                    )
+                cols = slice(c * P, (c + 1) * P)
+                for il in range(IL):
+                    nc.vector.quantize_mx(
+                        out=enc_codes[:, il, cols].bitcast(FP8X4),
+                        scales=enc_scales[:, il, cols],
+                        in_=e_grp[:, il * P * PACK : (il + 1) * P * PACK],
+                    )
             nc.vector.tensor_copy(
                 out=z_codes[:, 0 : O * D * P].bitcast(I32).rearrange("p (g c) -> p g c", c=P)[:, :, ZERO_COLS:P],
                 in_=w_codes[:].bitcast(I32).rearrange("p (g k) -> p g k", k=LS),
@@ -123,117 +167,99 @@ def tile_localcrossattention_pa_t_kernel(tc, scores, final_encoder_out, WV_w, WV
                     out=z_scale_words[:, :, il, :],
                     in_=w_scales[:].bitcast(I32).rearrange("p (g w) -> p g w", w=LS // 4),
                 )
+            load_scores(1)
+            load_scores(2)
 
+        attn_pool = stack.enter_context(tc.tile_pool(name="attn", bufs=3))
+        a_stage = stack.enter_context(tc.tile_pool(name="a_stage", bufs=2))
+        a_keep = stack.enter_context(tc.tile_pool(name="a_keep", bufs=4))
         v_stage = stack.enter_context(tc.tile_pool(name="v_stage", bufs=2))
-        v_keep = stack.enter_context(tc.tile_pool(name="v_keep", bufs=6))
+        v_keep = stack.enter_context(tc.tile_pool(name="v_keep", bufs=4))
+        res_pool = stack.enter_context(tc.tile_pool(name="res", bufs=2))
 
-        enc_codes = const.tile([P, IL, B * IH], U32, align_bytes=64)
-        enc_scales = const.tile([P, IL, B * IH], U8, align_bytes=64)
+        sums_of = {}
+        denom_of = {}
+        recip_of = {}
+        attn_of = {}
 
-        def prepare_enc(c):
-            e_nat = enc_stage.tile([P, IL * FS], BF16)
-            nc.sync.dma_start(out=e_nat[:], in_=enc_rows[c * P : (c + 1) * P, :])
-            e_words = e_nat[:].bitcast(F32)
-            e_grp = enc_stage.tile([P, IL * P * PACK], BF16, align_bytes=64)
-            e_grp_words = e_grp[:].bitcast(F32).rearrange("p (l m u) -> p l m u", l=IL, u=2)
-            for pair in range(IL // 2):
-                et = ps_words.tile([P, 2, 2, P], F32, name="et", tag="words")
-                for li in range(2):
-                    for u in range(2):
-                        first = ((2 * pair + li) * 2 + u) * P
-                        nc.tensor.transpose(
-                            out=et[:, li, u, :], in_=e_words[:, first : first + P], identity=ident_f32[:]
-                        )
-                nc.vector.tensor_copy(
-                    out=e_grp_words[:, 2 * pair : 2 * pair + 2, :, :],
-                    in_=et[:].rearrange("p l u m -> p l m u"),
-                )
-            cols = slice(c * P, (c + 1) * P)
-            for il in range(IL):
-                nc.vector.quantize_mx(
-                    out=enc_codes[:, il, cols].bitcast(FP8X4),
-                    scales=enc_scales[:, il, cols],
-                    in_=e_grp[:, il * P * PACK : (il + 1) * P * PACK],
-                )
+        def sum_keys(h):
+            sums = sum_pool.tile([P, GROUPS], F32, name="sums", tag="sums")
+            nc.vector.tensor_reduce(
+                out=sums[:],
+                in_=e_tiles[h][:].rearrange("p (g k) -> p g k", k=LS),
+                axis=mybir.AxisListType.X,
+                op=ALU.add,
+            )
+            sums_of[h] = sums
 
-        prepare_enc(0)
-        prepare_enc(1)
-        load_scores(1)
+        def add_eps(h):
+            denom = sum_pool.tile([P, GROUPS], F32, name="denom", tag="denom")
+            nc.vector.tensor_scalar_add(out=denom[:], in0=sums_of[h][:], scalar1=EPS)
+            denom_of[h] = denom
 
-        attn_tiles = {}
+        def invert(h):
+            recip = sum_pool.tile([P, GROUPS], F32, name="recip", tag="recip")
+            nc.vector.reciprocal(out=recip[:], in_=denom_of[h][:])
+            recip_of[h] = recip
 
-        def softmax(g):
-            x_by_query = x_tiles[g][:].rearrange("p (l q k) -> p q l k", l=IL, q=LQ)
-            attn = attn_pool.tile([P, ROW], BF16)
-            for half in range(LQ // HALF_Q):
-                groups = HALF_Q * IL
-                e = e_pool.tile([P, groups * LS], F32)
-                nc.scalar.activation(
-                    out=e[:].rearrange("p (q l k) -> p q l k", l=IL, k=LS),
-                    in_=x_by_query[:, half * HALF_Q : (half + 1) * HALF_Q],
-                    func=ACT.Exp,
-                )
-                e_groups = e[:].rearrange("p (g k) -> p g k", k=LS)
-                sums = sum_pool.tile([P, groups], F32)
-                nc.vector.tensor_reduce(out=sums[:], in_=e_groups, axis=mybir.AxisListType.X, op=ALU.add)
-                denom = sum_pool.tile([P, groups], F32)
-                nc.vector.tensor_scalar_add(out=denom[:], in0=sums[:], scalar1=EPS)
-                recip = sum_pool.tile([P, groups], F32)
-                nc.vector.reciprocal(out=recip[:], in_=denom[:])
-                attn_groups = attn[:, half * groups * LS : (half + 1) * groups * LS].rearrange(
-                    "p (g k) -> p g k", k=LS
-                )
-                split = groups - GPSIMD_GROUPS
-                nc.vector.tensor_tensor(
-                    out=attn_groups[:, 0:split, :],
-                    in0=e_groups[:, 0:split, :],
-                    in1=recip[:, 0:split].unsqueeze(2).to_broadcast([P, split, LS]),
-                    op=ALU.mult,
-                )
-                nc.gpsimd.tensor_tensor(
-                    out=attn_groups[:, split:groups, :],
-                    in0=e_groups[:, split:groups, :],
-                    in1=recip[:, split:groups].unsqueeze(2).to_broadcast([P, GPSIMD_GROUPS, LS]),
-                    op=ALU.mult,
-                )
-            attn_tiles[g] = attn
+        def normalise(h):
+            attn = attn_pool.tile([P, HALF], BF16, name="attn", tag="attn")
+            nc.vector.tensor_tensor(
+                out=attn[:].rearrange("p (g k) -> p g k", k=LS),
+                in0=e_tiles[h][:].rearrange("p (g k) -> p g k", k=LS),
+                in1=recip_of[h][:].unsqueeze(2).to_broadcast([P, GROUPS, LS]),
+                op=ALU.mult,
+            )
+            attn_of[h] = attn
 
+        banks_of = {}
+        a_grp_of = {}
         attn_q = {}
 
-        def transpose_and_quantise(g):
-            attn = attn_tiles[g]
-            a_grp = a_stage.tile([P, ROW], BF16, align_bytes=64)
-            a_grp_banks = a_grp[:].rearrange("p (c n x) -> p c n x", n=LQ // BANK_Q, x=BANK_Q * PACK)
-            for bank in range(LQ // BANK_Q):
-                at = ps_attn.tile([P, O * TILE_B * BANK_Q * PACK], BF16)
+        def transpose(h):
+            banks_of[h] = []
+            for bank in range(HALF_BANKS):
+                at = ps_t.tile([P, O * TILE_B * BANK_Q * PACK], BF16, name="at", tag="t")
                 at_by_query = at[:].rearrange("p (o b q t) -> p b o q t", o=O, b=TILE_B, q=BANK_Q)
                 for qi in range(BANK_Q):
                     q = bank * BANK_Q + qi
                     nc.tensor.transpose(
-                        out=at_by_query[:, :, :, qi, :], in_=attn[:, q * P : (q + 1) * P], identity=ident_bf[:]
+                        out=at_by_query[:, :, :, qi, :],
+                        in_=attn_of[h][:, q * P : (q + 1) * P],
+                        identity=ident_bf[:],
                     )
+                banks_of[h].append(at)
+
+        def copy_out(h):
+            g, half = divmod(h, 2)
+            if half == 0:
+                a_grp_of[g] = a_stage.tile([P, ROW], BF16, name="a_grp", tag="a_grp", align_bytes=64)
+            a_grp_banks = a_grp_of[g][:].rearrange(
+                "p (c n x) -> p c n x", n=LQ // BANK_Q, x=BANK_Q * PACK
+            )
+            for bank in range(HALF_BANKS):
                 nc.scalar.copy(
-                    out=a_grp_banks[:, :, bank, :],
-                    in_=at[:].rearrange("p (c x) -> p c x", x=BANK_Q * PACK),
+                    out=a_grp_banks[:, :, half * HALF_BANKS + bank, :],
+                    in_=banks_of[h][bank][:].rearrange("p (c x) -> p c x", x=BANK_Q * PACK),
                 )
+
+        def quantise_attn(g):
             a_codes = a_keep.tile([P, ROW // PACK], U32, name="a_codes", tag="a_codes", align_bytes=64)
             a_scales = a_keep.tile([P, ROW // PACK], U8, name="a_scales", tag="a_scales", align_bytes=64)
-            nc.vector.quantize_mx(out=a_codes[:].bitcast(FP8X4), scales=a_scales[:], in_=a_grp[:])
+            nc.vector.quantize_mx(out=a_codes[:].bitcast(FP8X4), scales=a_scales[:], in_=a_grp_of[g][:])
             attn_q[g] = (a_codes, a_scales)
 
+        v_grp_of = {}
         v_q = {}
-        v_grps = {}
-        v_cols = QUARTER_B // GROUP_B * D * GROUP_B
 
         def project_pair(quarter, o, d_pair):
             if d_pair == 0:
-                v_grps[(quarter, o)] = v_stage.tile(
-                    [P, v_cols * PACK], BF16, name="v_grp", tag="v_grp", align_bytes=64
+                v_grp_of[(quarter, o)] = v_stage.tile(
+                    [P, V_COLS * PACK], BF16, name="v_grp", tag="v_grp", align_bytes=64
                 )
-            v_grp = v_grps[(quarter, o)]
-            v_grp_by_d = v_grp[:].rearrange("p (n d x) -> p n d x", d=D, x=GROUP_B * PACK)
+            v_grp_by_d = v_grp_of[(quarter, o)][:].rearrange("p (n d x) -> p n d x", d=D, x=GROUP_B * PACK)
             cols = slice(quarter * QUARTER_COLS, (quarter + 1) * QUARTER_COLS)
-            acc = ps_v.tile([P, 2, QUARTER_COLS], F32)
+            acc = ps_v.tile([P, 2, QUARTER_COLS], F32, name="acc", tag="acc")
             for di in range(2):
                 od = o * D + 2 * d_pair + di
                 for il in range(IL):
@@ -255,44 +281,50 @@ def tile_localcrossattention_pa_t_kernel(tc, scores, final_encoder_out, WV_w, WV
                     func=ACT.Identity,
                     bias=bias_col[:, o * D + d : o * D + d + 1],
                 )
-            if d_pair == D // 2 - 1:
-                v_codes = v_keep.tile([P, v_cols], U32, name="v_codes", tag="v_codes", align_bytes=64)
-                v_scales = v_keep.tile([P, v_cols], U8, name="v_scales", tag="v_scales", align_bytes=64)
-                nc.vector.quantize_mx(out=v_codes[:].bitcast(FP8X4), scales=v_scales[:], in_=v_grp[:])
-                v_q[(quarter, o)] = (v_codes, v_scales)
 
-        res_tiles = {}
-        pass_cols = D * GROUP_B
+        def quantise_v(quarter, o):
+            v_codes = v_keep.tile([P, V_COLS], U32, name="v_codes", tag="v_codes", align_bytes=64)
+            v_scales = v_keep.tile([P, V_COLS], U8, name="v_scales", tag="v_scales", align_bytes=64)
+            nc.vector.quantize_mx(
+                out=v_codes[:].bitcast(FP8X4), scales=v_scales[:], in_=v_grp_of[(quarter, o)][:]
+            )
+            v_q[(quarter, o)] = (v_codes, v_scales)
+
+        o_acc_of = {}
+        res_of = {}
 
         def attend(g):
             quarter, gi = divmod(g, QUARTER_TILES)
-            groups = TILE_B // GROUP_B
             a_codes, a_scales = attn_q[g]
-            o_acc = ps_out.tile([P, O, groups, D, GROUP_B], F32)
+            o_acc = ps_out.tile([P, O, TILE_GROUPS, D, GROUP_B], F32, name="o_acc", tag="o_acc")
             for o in range(O):
                 v_codes, v_scales = v_q[(quarter, o)]
-                for s in range(groups):
-                    a_cols = slice((o * groups + s) * P, (o * groups + s + 1) * P)
-                    v_first = (gi * groups + s) * pass_cols
+                for s in range(TILE_GROUPS):
+                    a_cols = slice((o * TILE_GROUPS + s) * P, (o * TILE_GROUPS + s + 1) * P)
+                    v_cols = slice((gi * TILE_GROUPS + s) * PASS_COLS, (gi * TILE_GROUPS + s + 1) * PASS_COLS)
                     nc.tensor.matmul_mx(
                         out=o_acc[:, o, s].rearrange("p d j -> p (d j)"),
                         lhsT=a_codes[:, a_cols].bitcast(FP8X4),
                         lhsT_scale=a_scales[:, a_cols],
-                        rhs=v_codes[:, v_first : v_first + pass_cols].bitcast(FP8X4),
-                        rhs_scale=v_scales[:, v_first : v_first + pass_cols],
+                        rhs=v_codes[:, v_cols].bitcast(FP8X4),
+                        rhs_scale=v_scales[:, v_cols],
                         start=True,
                         stop=True,
                     )
+            o_acc_of[g] = o_acc
+
+        def pick_and_store(g):
+            quarter, gi = divmod(g, QUARTER_TILES)
             if gi == 0:
-                res_tiles[quarter] = res_pool.tile(
-                    [P, O, QUARTER_TILES, groups, D], F32, name="res", tag="res"
+                res_of[quarter] = res_pool.tile(
+                    [P, O, QUARTER_TILES, TILE_GROUPS, D], F32, name="res", tag="res"
                 )
-            res = res_tiles[quarter]
+            res = res_of[quarter]
             for j in range(GROUP_B):
                 rows = slice(j * LQ, (j + 1) * LQ)
-                nc.scalar.mul(out=res[rows, :, gi, :, :], in_=o_acc[rows, :, :, :, j], mul=1.0 / 4.0)
+                nc.scalar.mul(out=res[rows, :, gi, :, :], in_=o_acc_of[g][rows, :, :, :, j], mul=1.0 / 4.0)
             if gi == QUARTER_TILES - 1:
-                n_groups = QUARTER_TILES * groups
+                n_groups = QUARTER_TILES * TILE_GROUPS
                 for j in range(GROUP_B):
                     for o in range(O):
                         nc.sync.dma_start(
@@ -300,20 +332,49 @@ def tile_localcrossattention_pa_t_kernel(tc, scores, final_encoder_out, WV_w, WV
                             in_=res[j * LQ : (j + 1) * LQ, o].rearrange("q g s d -> q (g s) d"),
                         )
 
-        pairs = [(quarter, o, d_pair) for quarter in range(QUARTERS) for o in range(O) for d_pair in range(D // 2)]
-        pairs_of_a_quarter = O * D // 2
-        pairs_done = 0
+        pairs = [(quarter, o, d_pair) for quarter in range(QUARTERS) for o in range(O) for d_pair in range(D_PAIRS)]
+        projected = 0
+        v_quantised = 0
+        attn_quantised = 0
         attended = 0
-        for g in range(TILES):
-            if g + 2 < TILES:
-                load_scores(g + 2)
-            softmax(g)
-            transpose_and_quantise(g)
-            if g + 2 < ENC_CHUNKS:
-                prepare_enc(g + 2)
-            for quarter, o, d_pair in pairs[pairs_done : pairs_done + PAIRS_PER_TILE]:
+        picked = 0
+        n = 0
+        while picked < TILES:
+            projected_before, v_before, attn_before, attended_before = (
+                projected,
+                v_quantised,
+                attn_quantised,
+                attended,
+            )
+            if 2 <= n + 1 < HALVES:
+                exp(n + 1)
+            if n % 2 == 0 and n // 2 + 3 < TILES:
+                load_scores(n // 2 + 3)
+            if 0 <= n - 1 < HALVES:
+                add_eps(n - 1)
+            if n < HALVES:
+                sum_keys(n)
+            if 0 <= n - 1 < HALVES:
+                invert(n - 1)
+            if 0 <= n - 2 < HALVES:
+                normalise(n - 2)
+            for quarter, o, d_pair in pairs[projected : projected + PAIRS_PER_STEP]:
                 project_pair(quarter, o, d_pair)
-            pairs_done = min(pairs_done + PAIRS_PER_TILE, len(pairs))
-            while attended <= g and attended // QUARTER_TILES < pairs_done // pairs_of_a_quarter:
+            projected = min(projected + PAIRS_PER_STEP, len(pairs))
+            if 0 <= n - 3 < HALVES:
+                transpose(n - 3)
+            if 0 <= n - 4 < HALVES:
+                copy_out(n - 4)
+            while picked < attended_before:
+                pick_and_store(picked)
+                picked += 1
+            if n >= 6 and n % 2 == 0 and attn_quantised < TILES:
+                quantise_attn(attn_quantised)
+                attn_quantised += 1
+            while v_quantised < projected_before // D_PAIRS:
+                quantise_v(v_quantised // O, v_quantised % O)
+                v_quantised += 1
+            while attended < attn_before and O * (attended // QUARTER_TILES + 1) <= v_before:
                 attend(attended)
                 attended += 1
+            n += 1

@@ -30,6 +30,7 @@ GROUPS = HALF_Q * IL
 HALF = GROUPS * LS
 BANK_Q = 8
 HALF_BANKS = HALF_Q // BANK_Q
+GPSIMD_GROUPS = 32
 
 QUARTERS = 4
 QUARTER_B = B // QUARTERS
@@ -202,15 +203,18 @@ def tile_localcrossattention_pa_t_kernel(tc, scores, final_encoder_out, WV_w, WV
             nc.vector.reciprocal(out=recip[:], in_=denom_of[h][:])
             recip_of[h] = recip
 
-        def normalise(h):
+        def new_attn(h):
             attn = attn_pool.tile([P, HALF], BF16, name="attn", tag="attn")
-            nc.vector.tensor_tensor(
-                out=attn[:].rearrange("p (g k) -> p g k", k=LS),
-                in0=e_tiles[h][:].rearrange("p (g k) -> p g k", k=LS),
-                in1=recip_of[h][:].unsqueeze(2).to_broadcast([P, GROUPS, LS]),
+            attn_of[h] = attn
+
+        def multiply(engine, h, first, count):
+            groups = slice(first, first + count)
+            engine.tensor_tensor(
+                out=attn_of[h][:].rearrange("p (g k) -> p g k", k=LS)[:, groups, :],
+                in0=e_tiles[h][:].rearrange("p (g k) -> p g k", k=LS)[:, groups, :],
+                in1=recip_of[h][:, groups].unsqueeze(2).to_broadcast([P, count, LS]),
                 op=ALU.mult,
             )
-            attn_of[h] = attn
 
         banks_of = {}
         a_grp_of = {}
@@ -350,6 +354,9 @@ def tile_localcrossattention_pa_t_kernel(tc, scores, final_encoder_out, WV_w, WV
                 exp(n + 1)
             if n % 2 == 0 and n // 2 + 3 < TILES:
                 load_scores(n // 2 + 3)
+            if 0 <= n - 2 < HALVES:
+                new_attn(n - 2)
+                multiply(nc.gpsimd, n - 2, GROUPS - GPSIMD_GROUPS, GPSIMD_GROUPS)
             if 0 <= n - 1 < HALVES:
                 add_eps(n - 1)
             if n < HALVES:
@@ -357,7 +364,7 @@ def tile_localcrossattention_pa_t_kernel(tc, scores, final_encoder_out, WV_w, WV
             if 0 <= n - 1 < HALVES:
                 invert(n - 1)
             if 0 <= n - 2 < HALVES:
-                normalise(n - 2)
+                multiply(nc.vector, n - 2, 0, GROUPS - GPSIMD_GROUPS)
             for quarter, o, d_pair in pairs[projected : projected + PAIRS_PER_STEP]:
                 project_pair(quarter, o, d_pair)
             projected = min(projected + PAIRS_PER_STEP, len(pairs))

@@ -30,7 +30,9 @@ GROUPS = HALF_Q * IL
 HALF = GROUPS * LS
 BANK_Q = 8
 HALF_BANKS = HALF_Q // BANK_Q
-GPSIMD_GROUPS = 32
+TILE_BANKS = LQ // BANK_Q
+GPSIMD_GROUPS = 40
+VECTOR_BANK = TILE_BANKS - 1
 
 QUARTERS = 4
 QUARTER_B = B // QUARTERS
@@ -43,8 +45,12 @@ PASS_COLS = D * GROUP_B
 V_COLS = QUARTER_B * D
 ZERO_COLS = P - LS
 D_PAIRS = D // 2
+OUT_BANKS = 2
 
 PAIRS_PER_STEP = 2
+FIRST_PAIR_STEP = 2
+ENC_PER_STEP = 2
+WARMUP_STEPS = ENC_CHUNKS // ENC_PER_STEP + 1
 
 
 def tile_localcrossattention_pa_t_kernel(tc, scores, final_encoder_out, WV_w, WV_b, out):
@@ -61,14 +67,26 @@ def tile_localcrossattention_pa_t_kernel(tc, scores, final_encoder_out, WV_w, WV
         x_pool = stack.enter_context(tc.tile_pool(name="x", bufs=3))
         e_pool = stack.enter_context(tc.tile_pool(name="e", bufs=5))
         sum_pool = stack.enter_context(tc.tile_pool(name="sums", bufs=4))
+        attn_pool = stack.enter_context(tc.tile_pool(name="attn", bufs=3))
+        a_stage = stack.enter_context(tc.tile_pool(name="a_stage", bufs=2))
+        v_stage = stack.enter_context(tc.tile_pool(name="v_stage", bufs=2))
+        v_keep = stack.enter_context(tc.tile_pool(name="v_keep", bufs=4))
         ps_t = stack.enter_context(tc.psum_pool(name="ps_t", bufs=4))
         ps_v = stack.enter_context(tc.psum_pool(name="ps_v", bufs=2))
-        ps_out = stack.enter_context(tc.psum_pool(name="ps_out", bufs=2))
+        ps_out = stack.enter_context(tc.psum_pool(name="ps_out", bufs=OUT_BANKS))
 
-        ident_bf = const.tile([P, P], BF16)
-        make_identity(nc, ident_bf[:])
         ident_f32 = const.tile([P, P], F32)
         make_identity(nc, ident_f32[:])
+        ident_bf = const.tile([P, P], BF16)
+        make_identity(nc, ident_bf[:])
+
+        z_codes = const.tile([P, O * D * P + ZERO_COLS], U32, align_bytes=64)
+        nc.vector.memset(z_codes[:].bitcast(I32), 0)
+        z_scales = const.tile([P, O * D * P], U8, align_bytes=64)
+        enc_codes = const.tile([P, IL, B * IH], U32, align_bytes=64)
+        enc_scales = const.tile([P, IL, B * IH], U8, align_bytes=64)
+        bias_bf = const.tile([P, O * D], BF16)
+        bias_col = const.tile([P, O * D], F32)
 
         x_tiles = {}
         e_tiles = {}
@@ -89,95 +107,6 @@ def tile_localcrossattention_pa_t_kernel(tc, scores, final_encoder_out, WV_w, WV
             )
             e_tiles[h] = e
 
-        load_scores(0)
-        exp(0)
-        exp(1)
-
-        bias_bf = const.tile([P, O * D], BF16)
-        for il in range(IL):
-            nc.sync.dma_start(
-                out=bias_bf[il * LS : (il + 1) * LS, :].rearrange("k (o d) -> k o d", o=O),
-                in_=WV_b.rearrange("o (k d) -> k o d", d=D),
-            )
-        bias_col = const.tile([P, O * D], F32)
-
-        z_codes = const.tile([P, O * D * P + ZERO_COLS], U32, align_bytes=64)
-        nc.vector.memset(z_codes[:].bitcast(I32), 0)
-        z_scales = const.tile([P, O * D * P], U8, align_bytes=64)
-        enc_codes = const.tile([P, IL, B * IH], U32, align_bytes=64)
-        enc_scales = const.tile([P, IL, B * IH], U8, align_bytes=64)
-
-        with tc.tile_pool(name="w_prep", bufs=1) as w_prep, tc.tile_pool(name="enc_stage", bufs=2) as enc_stage:
-            w_nat = w_prep.tile([P, O * FS // P, FS], BF16)
-            nc.sync.dma_start(out=w_nat[:], in_=w_rows)
-            w_scales = w_prep.tile([P, O * FS], U8, align_bytes=64)
-            nc.vector.memset(w_scales[:].bitcast(I32), 0)
-            nc.vector.tensor_copy(out=bias_col[:], in_=bias_bf[:])
-            w_grp = w_prep.tile([P, O * FS * PACK], BF16, align_bytes=64)
-            w_grp_words = w_grp[:].bitcast(F32).rearrange("p (o d k u) -> p o d k u", o=O, d=D, k=LS)
-            k_rows = P // D
-            for pair in range(O * FS // P // 2):
-                wt = ps_t.tile([P, 2, 2, P], F32, name="wt", tag="t")
-                for ci in range(2):
-                    w_words = w_nat[:, 2 * pair + ci, :].bitcast(F32)
-                    for u in range(2):
-                        nc.tensor.transpose(
-                            out=wt[:, ci, u, :], in_=w_words[:, u * P : (u + 1) * P], identity=ident_f32[:]
-                        )
-                for ci in range(2):
-                    o, kc = divmod(2 * pair + ci, LS // k_rows)
-                    nc.scalar.copy(
-                        out=w_grp_words[:, o, :, kc * k_rows : (kc + 1) * k_rows, :],
-                        in_=wt[:, ci].rearrange("p u (k d) -> p d k u", d=D),
-                    )
-            w_codes = w_prep.tile([P, O * FS], U32, align_bytes=64)
-            nc.vector.quantize_mx(out=w_codes[:].bitcast(FP8X4), scales=w_scales[:], in_=w_grp[:])
-
-            for c in range(ENC_CHUNKS):
-                e_nat = enc_stage.tile([P, IL * FS], BF16, bufs=4)
-                nc.sync.dma_start(out=e_nat[:], in_=enc_rows[c * P : (c + 1) * P, :])
-                e_words = e_nat[:].bitcast(F32)
-                e_grp = enc_stage.tile([P, IL * P * PACK], BF16, align_bytes=64)
-                e_grp_words = e_grp[:].bitcast(F32).rearrange("p (l m u) -> p l m u", l=IL, u=2)
-                for pair in range(IL // 2):
-                    et = ps_t.tile([P, 2, 2, P], F32, name="et", tag="t")
-                    for li in range(2):
-                        for u in range(2):
-                            first = ((2 * pair + li) * 2 + u) * P
-                            nc.tensor.transpose(
-                                out=et[:, li, u, :], in_=e_words[:, first : first + P], identity=ident_f32[:]
-                            )
-                    nc.scalar.copy(
-                        out=e_grp_words[:, 2 * pair : 2 * pair + 2, :, :],
-                        in_=et[:].rearrange("p l u m -> p l m u"),
-                    )
-                cols = slice(c * P, (c + 1) * P)
-                for il in range(IL):
-                    nc.vector.quantize_mx(
-                        out=enc_codes[:, il, cols].bitcast(FP8X4),
-                        scales=enc_scales[:, il, cols],
-                        in_=e_grp[:, il * P * PACK : (il + 1) * P * PACK],
-                    )
-            nc.vector.tensor_copy(
-                out=z_codes[:, 0 : O * D * P].bitcast(I32).rearrange("p (g c) -> p g c", c=P)[:, :, ZERO_COLS:P],
-                in_=w_codes[:].bitcast(I32).rearrange("p (g k) -> p g k", k=LS),
-            )
-            z_scale_words = z_scales[:].bitcast(I32).rearrange("p (g r w) -> p g r w", r=IL, w=LS // 4)
-            for il in range(IL):
-                nc.vector.tensor_copy(
-                    out=z_scale_words[:, :, il, :],
-                    in_=w_scales[:].bitcast(I32).rearrange("p (g w) -> p g w", w=LS // 4),
-                )
-            load_scores(1)
-            load_scores(2)
-
-        attn_pool = stack.enter_context(tc.tile_pool(name="attn", bufs=3))
-        a_stage = stack.enter_context(tc.tile_pool(name="a_stage", bufs=2))
-        a_keep = stack.enter_context(tc.tile_pool(name="a_keep", bufs=4))
-        v_stage = stack.enter_context(tc.tile_pool(name="v_stage", bufs=2))
-        v_keep = stack.enter_context(tc.tile_pool(name="v_keep", bufs=4))
-        res_pool = stack.enter_context(tc.tile_pool(name="res", bufs=2))
-
         sums_of = {}
         denom_of = {}
         recip_of = {}
@@ -195,7 +124,7 @@ def tile_localcrossattention_pa_t_kernel(tc, scores, final_encoder_out, WV_w, WV
 
         def add_eps(h):
             denom = sum_pool.tile([P, GROUPS], F32, name="denom", tag="denom")
-            nc.vector.tensor_scalar_add(out=denom[:], in0=sums_of[h][:], scalar1=EPS)
+            nc.gpsimd.tensor_scalar_add(out=denom[:], in0=sums_of[h][:], scalar1=EPS)
             denom_of[h] = denom
 
         def invert(h):
@@ -234,18 +163,18 @@ def tile_localcrossattention_pa_t_kernel(tc, scores, final_encoder_out, WV_w, WV
                     )
                 banks_of[h].append(at)
 
-        def copy_out(h):
-            g, half = divmod(h, 2)
-            if half == 0:
-                a_grp_of[g] = a_stage.tile([P, ROW], BF16, name="a_grp", tag="a_grp", align_bytes=64)
+        def new_a_grp(g):
+            a_grp_of[g] = a_stage.tile([P, ROW], BF16, name="a_grp", tag="a_grp", align_bytes=64)
+
+        def copy_bank(copy, g, tile_bank):
+            half, bank = divmod(tile_bank, HALF_BANKS)
             a_grp_banks = a_grp_of[g][:].rearrange(
-                "p (c n x) -> p c n x", n=LQ // BANK_Q, x=BANK_Q * PACK
+                "p (c n x) -> p c n x", n=TILE_BANKS, x=BANK_Q * PACK
             )
-            for bank in range(HALF_BANKS):
-                nc.scalar.copy(
-                    out=a_grp_banks[:, :, half * HALF_BANKS + bank, :],
-                    in_=banks_of[h][bank][:].rearrange("p (c x) -> p c x", x=BANK_Q * PACK),
-                )
+            copy(
+                out=a_grp_banks[:, :, tile_bank, :],
+                in_=banks_of[2 * g + half][bank][:].rearrange("p (c x) -> p c x", x=BANK_Q * PACK),
+            )
 
         def quantise_attn(g):
             a_codes = a_keep.tile([P, ROW // PACK], U32, name="a_codes", tag="a_codes", align_bytes=64)
@@ -336,52 +265,167 @@ def tile_localcrossattention_pa_t_kernel(tc, scores, final_encoder_out, WV_w, WV
                             in_=res[j * LQ : (j + 1) * LQ, o].rearrange("q g s d -> q (g s) d"),
                         )
 
+        e_nat_of = {}
+        e_grp_of = {}
+
+        def load_enc(c):
+            e_nat = enc_stage.tile([P, IL * FS], BF16, name="e_nat", tag="e_nat")
+            nc.sync.dma_start(out=e_nat[:], in_=enc_rows[c * P : (c + 1) * P, :])
+            e_nat_of[c] = e_nat
+
+        def transpose_enc(c):
+            e_words = e_nat_of[c][:].bitcast(F32)
+            e_grp = enc_stage.tile([P, IL * P * PACK], BF16, name="e_grp", tag="e_grp", align_bytes=64)
+            e_grp_words = e_grp[:].bitcast(F32).rearrange("p (l m u) -> p l m u", l=IL, u=2)
+            for pair in range(IL // 2):
+                et = ps_t.tile([P, 2, 2, P], F32, name="et", tag="t")
+                for li in range(2):
+                    for u in range(2):
+                        first = ((2 * pair + li) * 2 + u) * P
+                        nc.tensor.transpose(
+                            out=et[:, li, u, :], in_=e_words[:, first : first + P], identity=ident_f32[:]
+                        )
+                nc.scalar.copy(
+                    out=e_grp_words[:, 2 * pair : 2 * pair + 2, :, :],
+                    in_=et[:].rearrange("p l u m -> p l m u"),
+                )
+            e_grp_of[c] = e_grp
+
+        def quantise_enc(c):
+            cols = slice(c * P, (c + 1) * P)
+            for il in range(IL):
+                nc.vector.quantize_mx(
+                    out=enc_codes[:, il, cols].bitcast(FP8X4),
+                    scales=enc_scales[:, il, cols],
+                    in_=e_grp_of[c][:, il * P * PACK : (il + 1) * P * PACK],
+                )
+
         pairs = [(quarter, o, d_pair) for quarter in range(QUARTERS) for o in range(O) for d_pair in range(D_PAIRS)]
-        projected = 0
-        v_quantised = 0
-        attn_quantised = 0
-        attended = 0
-        picked = 0
-        n = 0
-        while picked < TILES:
-            projected_before, v_before, attn_before, attended_before = (
-                projected,
-                v_quantised,
-                attn_quantised,
-                attended,
-            )
+        done = {
+            "enc": 0,
+            "enc_q": 0,
+            "pairs": 0,
+            "v_q": 0,
+            "attn_q": 0,
+            "attended": 0,
+            "picked": 0,
+        }
+
+        def step(n):
+            before = dict(done)
             if 2 <= n + 1 < HALVES:
                 exp(n + 1)
             if n % 2 == 0 and n // 2 + 3 < TILES:
                 load_scores(n // 2 + 3)
+            if 0 <= n - 1 < HALVES:
+                add_eps(n - 1)
             if 0 <= n - 2 < HALVES:
                 new_attn(n - 2)
                 multiply(nc.gpsimd, n - 2, GROUPS - GPSIMD_GROUPS, GPSIMD_GROUPS)
-            if 0 <= n - 1 < HALVES:
-                add_eps(n - 1)
             if n < HALVES:
                 sum_keys(n)
             if 0 <= n - 1 < HALVES:
                 invert(n - 1)
+            if 0 <= n - 4 < HALVES and (n - 4) % 2 == VECTOR_BANK // HALF_BANKS:
+                copy_bank(nc.vector.tensor_copy, (n - 4) // 2, VECTOR_BANK)
             if 0 <= n - 2 < HALVES:
                 multiply(nc.vector, n - 2, 0, GROUPS - GPSIMD_GROUPS)
-            for quarter, o, d_pair in pairs[projected : projected + PAIRS_PER_STEP]:
-                project_pair(quarter, o, d_pair)
-            projected = min(projected + PAIRS_PER_STEP, len(pairs))
+            if n >= FIRST_PAIR_STEP:
+                for quarter, o, d_pair in pairs[done["pairs"] : done["pairs"] + PAIRS_PER_STEP]:
+                    project_pair(quarter, o, d_pair)
+                done["pairs"] = min(done["pairs"] + PAIRS_PER_STEP, len(pairs))
+            for c in range(done["enc"], min(done["enc"] + ENC_PER_STEP, ENC_CHUNKS)):
+                transpose_enc(c)
+                if c + 2 * ENC_PER_STEP < ENC_CHUNKS:
+                    load_enc(c + 2 * ENC_PER_STEP)
+                done["enc"] = c + 1
             if 0 <= n - 3 < HALVES:
                 transpose(n - 3)
             if 0 <= n - 4 < HALVES:
-                copy_out(n - 4)
-            while picked < attended_before:
-                pick_and_store(picked)
-                picked += 1
-            if n >= 6 and n % 2 == 0 and attn_quantised < TILES:
-                quantise_attn(attn_quantised)
-                attn_quantised += 1
-            while v_quantised < projected_before // D_PAIRS:
-                quantise_v(v_quantised // O, v_quantised % O)
-                v_quantised += 1
-            while attended < attn_before and O * (attended // QUARTER_TILES + 1) <= v_before:
-                attend(attended)
-                attended += 1
+                g, half = divmod(n - 4, 2)
+                if half == 0:
+                    new_a_grp(g)
+                for bank in range(HALF_BANKS):
+                    if half * HALF_BANKS + bank != VECTOR_BANK:
+                        copy_bank(nc.scalar.copy, g, half * HALF_BANKS + bank)
+            while done["picked"] < before["attended"]:
+                pick_and_store(done["picked"])
+                done["picked"] += 1
+            while done["enc_q"] < before["enc"]:
+                quantise_enc(done["enc_q"])
+                done["enc_q"] += 1
+            if n >= 6 and n % 2 == 0 and done["attn_q"] < TILES:
+                quantise_attn(done["attn_q"])
+                done["attn_q"] += 1
+            while done["v_q"] < before["pairs"] // D_PAIRS:
+                quantise_v(done["v_q"] // O, done["v_q"] % O)
+                done["v_q"] += 1
+            for bank in range(OUT_BANKS):
+                g = done["attended"]
+                if g < before["attn_q"] and O * (g // QUARTER_TILES + 1) <= before["v_q"]:
+                    attend(g)
+                    done["attended"] += 1
+
+        with tc.tile_pool(name="w_prep", bufs=1) as w_prep, tc.tile_pool(
+            name="enc_stage", bufs=2 * ENC_PER_STEP
+        ) as enc_stage:
+            w_nat = w_prep.tile([P, O * FS // P, FS], BF16)
+            nc.sync.dma_start(out=w_nat[:], in_=w_rows)
+            load_scores(0)
+            for il in range(IL):
+                nc.sync.dma_start(
+                    out=bias_bf[il * LS : (il + 1) * LS, :].rearrange("k (o d) -> k o d", o=O),
+                    in_=WV_b.rearrange("o (k d) -> k o d", d=D),
+                )
+            load_enc(0)
+            load_enc(1)
+            load_scores(1)
+            load_enc(2)
+            load_enc(3)
+            load_scores(2)
+            exp(0)
+            exp(1)
+
+            w_scales = w_prep.tile([P, O * FS], U8, align_bytes=64)
+            nc.vector.memset(w_scales[:].bitcast(I32), 0)
+            w_grp = w_prep.tile([P, O * FS * PACK], BF16, align_bytes=64)
+            w_grp_words = w_grp[:].bitcast(F32).rearrange("p (o d k u) -> p o d k u", o=O, d=D, k=LS)
+            k_rows = P // D
+            for pair in range(O * FS // P // 2):
+                wt = ps_t.tile([P, 2, 2, P], F32, name="wt", tag="t")
+                for ci in range(2):
+                    w_words = w_nat[:, 2 * pair + ci, :].bitcast(F32)
+                    for u in range(2):
+                        nc.tensor.transpose(
+                            out=wt[:, ci, u, :], in_=w_words[:, u * P : (u + 1) * P], identity=ident_f32[:]
+                        )
+                for ci in range(2):
+                    o, kc = divmod(2 * pair + ci, LS // k_rows)
+                    nc.vector.tensor_copy(
+                        out=w_grp_words[:, o, :, kc * k_rows : (kc + 1) * k_rows, :],
+                        in_=wt[:, ci].rearrange("p u (k d) -> p d k u", d=D),
+                    )
+            nc.vector.tensor_copy(out=bias_col[:], in_=bias_bf[:])
+            w_codes = w_prep.tile([P, O * FS], U32, align_bytes=64)
+            nc.vector.quantize_mx(out=w_codes[:].bitcast(FP8X4), scales=w_scales[:], in_=w_grp[:])
+
+            step(0)
+            nc.vector.tensor_copy(
+                out=z_codes[:, 0 : O * D * P].bitcast(I32).rearrange("p (g c) -> p g c", c=P)[:, :, ZERO_COLS:P],
+                in_=w_codes[:].bitcast(I32).rearrange("p (g k) -> p g k", k=LS),
+            )
+            z_scale_words = z_scales[:].bitcast(I32).rearrange("p (g r w) -> p g r w", r=IL, w=LS // 4)
+            for il in range(IL):
+                nc.vector.tensor_copy(
+                    out=z_scale_words[:, :, il, :],
+                    in_=w_scales[:].bitcast(I32).rearrange("p (g w) -> p g w", w=LS // 4),
+                )
+            for n in range(1, WARMUP_STEPS):
+                step(n)
+
+        a_keep = stack.enter_context(tc.tile_pool(name="a_keep", bufs=4))
+        res_pool = stack.enter_context(tc.tile_pool(name="res", bufs=2))
+        n = WARMUP_STEPS
+        while done["picked"] < TILES:
+            step(n)
             n += 1

@@ -31,7 +31,7 @@ HALF = GROUPS * LS
 BANK_Q = 8
 HALF_BANKS = HALF_Q // BANK_Q
 TILE_BANKS = LQ // BANK_Q
-GPSIMD_GROUPS = 40
+GPSIMD_GROUPS = 36
 VECTOR_BANK = TILE_BANKS - 1
 
 QUARTERS = 4
@@ -124,7 +124,7 @@ def tile_localcrossattention_pa_t_kernel(tc, scores, final_encoder_out, WV_w, WV
 
         def add_eps(h):
             denom = sum_pool.tile([P, GROUPS], F32, name="denom", tag="denom")
-            nc.gpsimd.tensor_scalar_add(out=denom[:], in0=sums_of[h][:], scalar1=EPS)
+            nc.vector.tensor_scalar_add(out=denom[:], in0=sums_of[h][:], scalar1=EPS)
             denom_of[h] = denom
 
         def invert(h):
@@ -185,12 +185,9 @@ def tile_localcrossattention_pa_t_kernel(tc, scores, final_encoder_out, WV_w, WV
         v_grp_of = {}
         v_q = {}
 
+        acc_of = {}
+
         def project_pair(quarter, o, d_pair):
-            if d_pair == 0:
-                v_grp_of[(quarter, o)] = v_stage.tile(
-                    [P, V_COLS * PACK], BF16, name="v_grp", tag="v_grp", align_bytes=64
-                )
-            v_grp_by_d = v_grp_of[(quarter, o)][:].rearrange("p (n d x) -> p n d x", d=D, x=GROUP_B * PACK)
             cols = slice(quarter * QUARTER_COLS, (quarter + 1) * QUARTER_COLS)
             acc = ps_v.tile([P, 2, QUARTER_COLS], F32, name="acc", tag="acc")
             for di in range(2):
@@ -206,11 +203,19 @@ def tile_localcrossattention_pa_t_kernel(tc, scores, final_encoder_out, WV_w, WV
                         start=(il == 0),
                         stop=(il == IL - 1),
                     )
+            acc_of[(quarter, o, d_pair)] = acc
+
+        def add_bias_pair(quarter, o, d_pair):
+            if d_pair == 0:
+                v_grp_of[(quarter, o)] = v_stage.tile(
+                    [P, V_COLS * PACK], BF16, name="v_grp", tag="v_grp", align_bytes=64
+                )
+            v_grp_by_d = v_grp_of[(quarter, o)][:].rearrange("p (n d x) -> p n d x", d=D, x=GROUP_B * PACK)
             for di in range(2):
                 d = 2 * d_pair + di
                 nc.scalar.activation(
                     out=v_grp_by_d[:, :, d, :],
-                    in_=acc[:, di, :].rearrange("p (n x) -> p n x", x=GROUP_B * PACK),
+                    in_=acc_of[(quarter, o, d_pair)][:, di, :].rearrange("p (n x) -> p n x", x=GROUP_B * PACK),
                     func=ACT.Identity,
                     bias=bias_col[:, o * D + d : o * D + d + 1],
                 )
@@ -317,23 +322,22 @@ def tile_localcrossattention_pa_t_kernel(tc, scores, final_encoder_out, WV_w, WV
                 exp(n + 1)
             if n % 2 == 0 and n // 2 + 3 < TILES:
                 load_scores(n // 2 + 3)
-            if 0 <= n - 1 < HALVES:
-                add_eps(n - 1)
             if 0 <= n - 2 < HALVES:
                 new_attn(n - 2)
                 multiply(nc.gpsimd, n - 2, GROUPS - GPSIMD_GROUPS, GPSIMD_GROUPS)
+            if 0 <= n - 1 < HALVES:
+                add_eps(n - 1)
             if n < HALVES:
                 sum_keys(n)
-            if 0 <= n - 1 < HALVES:
-                invert(n - 1)
             if 0 <= n - 4 < HALVES and (n - 4) % 2 == VECTOR_BANK // HALF_BANKS:
                 copy_bank(nc.vector.tensor_copy, (n - 4) // 2, VECTOR_BANK)
+            if 0 <= n - 1 < HALVES:
+                invert(n - 1)
             if 0 <= n - 2 < HALVES:
                 multiply(nc.vector, n - 2, 0, GROUPS - GPSIMD_GROUPS)
             if n >= FIRST_PAIR_STEP:
                 for quarter, o, d_pair in pairs[done["pairs"] : done["pairs"] + PAIRS_PER_STEP]:
                     project_pair(quarter, o, d_pair)
-                done["pairs"] = min(done["pairs"] + PAIRS_PER_STEP, len(pairs))
             for c in range(done["enc"], min(done["enc"] + ENC_PER_STEP, ENC_CHUNKS)):
                 transpose_enc(c)
                 if c + 2 * ENC_PER_STEP < ENC_CHUNKS:
@@ -351,6 +355,10 @@ def tile_localcrossattention_pa_t_kernel(tc, scores, final_encoder_out, WV_w, WV
             while done["picked"] < before["attended"]:
                 pick_and_store(done["picked"])
                 done["picked"] += 1
+            if n >= FIRST_PAIR_STEP:
+                for quarter, o, d_pair in pairs[done["pairs"] : done["pairs"] + PAIRS_PER_STEP]:
+                    add_bias_pair(quarter, o, d_pair)
+                done["pairs"] = min(done["pairs"] + PAIRS_PER_STEP, len(pairs))
             while done["enc_q"] < before["enc"]:
                 quantise_enc(done["enc_q"])
                 done["enc_q"] += 1

@@ -255,19 +255,21 @@ def tile_localcrossattention_pa_t_kernel(tc, scores, final_encoder_out, WV_w, WV
             quarter, gi = divmod(g, QUARTER_TILES)
             if gi == 0:
                 res_of[quarter] = res_pool.tile(
-                    [P, O, QUARTER_TILES, TILE_GROUPS, D], F32, name="res", tag="res"
+                    [P, O, QUARTER_TILES, TILE_GROUPS, GROUP_B, D], F32, name="res", tag="res"
                 )
             res = res_of[quarter]
-            for j in range(GROUP_B):
-                rows = slice(j * LQ, (j + 1) * LQ)
-                nc.scalar.mul(out=res[rows, :, gi, :, :], in_=o_acc_of[g][rows, :, :, :, j], mul=1.0 / 4.0)
+            nc.scalar.mul(
+                out=res[:, :, gi],
+                in_=o_acc_of[g][:].rearrange("p o s d j -> p o s j d"),
+                mul=1.0 / 4.0,
+            )
             if gi == QUARTER_TILES - 1:
                 n_groups = QUARTER_TILES * TILE_GROUPS
                 for j in range(GROUP_B):
                     for o in range(O):
                         nc.sync.dma_start(
                             out=out_view[j, o, :, quarter * n_groups : (quarter + 1) * n_groups, :],
-                            in_=res[j * LQ : (j + 1) * LQ, o].rearrange("q g s d -> q (g s) d"),
+                            in_=res[j * LQ : (j + 1) * LQ, o, :, :, j, :].rearrange("q g s d -> q (g s) d"),
                         )
 
         e_nat_of = {}

@@ -34,11 +34,13 @@ TILE_BANKS = LQ // BANK_Q
 GPSIMD_GROUPS = 36
 VECTOR_BANK = TILE_BANKS - 1
 
+VECTOR_ONLY = 2
 QUARTERS = 4
 QUARTER_B = B // QUARTERS
 QUARTER_COLS = QUARTER_B * IH
 QUARTER_TILES = TILES // QUARTERS
 ENC_CHUNKS = B * IH // P
+QUARTER_CHUNKS = ENC_CHUNKS // QUARTERS
 GROUP_B = 4
 TILE_GROUPS = TILE_B // GROUP_B
 PASS_COLS = D * GROUP_B
@@ -83,8 +85,8 @@ def tile_localcrossattention_pa_t_kernel(tc, scores, final_encoder_out, WV_w, WV
         z_codes = const.tile([P, O * D * P + ZERO_COLS], U32, align_bytes=64)
         nc.vector.memset(z_codes[:].bitcast(I32), 0)
         z_scales = const.tile([P, O * D * P], U8, align_bytes=64)
-        enc_codes = const.tile([P, IL, B * IH], U32, align_bytes=64)
-        enc_scales = const.tile([P, IL, B * IH], U8, align_bytes=64)
+        enc_codes = const.tile([P, QUARTERS, IL, QUARTER_COLS], U32, align_bytes=64)
+        enc_scales = const.tile([P, QUARTERS, IL, QUARTER_COLS], U8, align_bytes=64)
         bias_bf = const.tile([P, O * D], BF16)
         bias_col = const.tile([P, O * D], F32)
 
@@ -188,7 +190,6 @@ def tile_localcrossattention_pa_t_kernel(tc, scores, final_encoder_out, WV_w, WV
         acc_of = {}
 
         def project_pair(quarter, o, d_pair):
-            cols = slice(quarter * QUARTER_COLS, (quarter + 1) * QUARTER_COLS)
             acc = ps_v.tile([P, 2, QUARTER_COLS], F32, name="acc", tag="acc")
             for di in range(2):
                 od = o * D + 2 * d_pair + di
@@ -198,8 +199,8 @@ def tile_localcrossattention_pa_t_kernel(tc, scores, final_encoder_out, WV_w, WV
                         out=acc[:, di, :],
                         lhsT=z_codes[:, first : first + P].bitcast(FP8X4),
                         lhsT_scale=z_scales[:, od * P : (od + 1) * P],
-                        rhs=enc_codes[:, il, cols].bitcast(FP8X4),
-                        rhs_scale=enc_scales[:, il, cols],
+                        rhs=enc_codes[:, quarter, il].bitcast(FP8X4),
+                        rhs_scale=enc_scales[:, quarter, il],
                         start=(il == 0),
                         stop=(il == IL - 1),
                     )
@@ -282,8 +283,13 @@ def tile_localcrossattention_pa_t_kernel(tc, scores, final_encoder_out, WV_w, WV
 
         def transpose_enc(c):
             e_words = e_nat_of[c][:].bitcast(F32)
-            e_grp = enc_stage.tile([P, IL * P * PACK], BF16, name="e_grp", tag="e_grp", align_bytes=64)
-            e_grp_words = e_grp[:].bitcast(F32).rearrange("p (l m u) -> p l m u", l=IL, u=2)
+            quarter, part = divmod(c, QUARTER_CHUNKS)
+            if part == 0:
+                e_grp_of[quarter] = enc_grp.tile(
+                    [P, IL * QUARTER_COLS * PACK], BF16, name="e_grp", tag="e_grp", align_bytes=64
+                )
+            e_grp_words = e_grp_of[quarter][:].bitcast(F32).rearrange("p (l m u) -> p l m u", l=IL, u=2)
+            rows = slice(part * P, (part + 1) * P)
             for pair in range(IL // 2):
                 et = ps_t.tile([P, 2, 2, P], F32, name="et", tag="t")
                 for li in range(2):
@@ -293,19 +299,16 @@ def tile_localcrossattention_pa_t_kernel(tc, scores, final_encoder_out, WV_w, WV
                             out=et[:, li, u, :], in_=e_words[:, first : first + P], identity=ident_f32[:]
                         )
                 nc.scalar.copy(
-                    out=e_grp_words[:, 2 * pair : 2 * pair + 2, :, :],
+                    out=e_grp_words[:, 2 * pair : 2 * pair + 2, rows, :],
                     in_=et[:].rearrange("p l u m -> p l m u"),
                 )
-            e_grp_of[c] = e_grp
 
-        def quantise_enc(c):
-            cols = slice(c * P, (c + 1) * P)
-            for il in range(IL):
-                nc.vector.quantize_mx(
-                    out=enc_codes[:, il, cols].bitcast(FP8X4),
-                    scales=enc_scales[:, il, cols],
-                    in_=e_grp_of[c][:, il * P * PACK : (il + 1) * P * PACK],
-                )
+        def quantise_enc(quarter):
+            nc.vector.quantize_mx(
+                out=enc_codes[:, quarter].rearrange("p l m -> p (l m)").bitcast(FP8X4),
+                scales=enc_scales[:, quarter].rearrange("p l m -> p (l m)"),
+                in_=e_grp_of[quarter][:],
+            )
 
         pairs = [(quarter, o, d_pair) for quarter in range(QUARTERS) for o in range(O) for d_pair in range(D_PAIRS)]
         done = {
@@ -326,17 +329,18 @@ def tile_localcrossattention_pa_t_kernel(tc, scores, final_encoder_out, WV_w, WV
                 load_scores(n // 2 + 3)
             if 0 <= n - 2 < HALVES:
                 new_attn(n - 2)
-                multiply(nc.gpsimd, n - 2, GROUPS - GPSIMD_GROUPS, GPSIMD_GROUPS)
+                if n - 2 < HALVES - VECTOR_ONLY:
+                    multiply(nc.gpsimd, n - 2, GROUPS - GPSIMD_GROUPS, GPSIMD_GROUPS)
             if 0 <= n - 1 < HALVES:
                 add_eps(n - 1)
             if n < HALVES:
                 sum_keys(n)
-            if 0 <= n - 4 < HALVES and (n - 4) % 2 == VECTOR_BANK // HALF_BANKS:
+            if 0 <= n - 4 < HALVES and (n - 4) % 2 == VECTOR_BANK // HALF_BANKS and (n - 4) // 2 < TILES - QUARTER_TILES:
                 copy_bank(nc.vector.tensor_copy, (n - 4) // 2, VECTOR_BANK)
             if 0 <= n - 1 < HALVES:
                 invert(n - 1)
             if 0 <= n - 2 < HALVES:
-                multiply(nc.vector, n - 2, 0, GROUPS - GPSIMD_GROUPS)
+                multiply(nc.vector, n - 2, 0, GROUPS - GPSIMD_GROUPS if n - 2 < HALVES - VECTOR_ONLY else GROUPS)
             if n >= FIRST_PAIR_STEP:
                 for quarter, o, d_pair in pairs[done["pairs"] : done["pairs"] + PAIRS_PER_STEP]:
                     project_pair(quarter, o, d_pair)
@@ -352,7 +356,7 @@ def tile_localcrossattention_pa_t_kernel(tc, scores, final_encoder_out, WV_w, WV
                 if half == 0:
                     new_a_grp(g)
                 for bank in range(HALF_BANKS):
-                    if half * HALF_BANKS + bank != VECTOR_BANK:
+                    if half * HALF_BANKS + bank != VECTOR_BANK or not (g < TILES - QUARTER_TILES):
                         copy_bank(nc.scalar.copy, g, half * HALF_BANKS + bank)
             while done["picked"] < before["attended"]:
                 pick_and_store(done["picked"])
@@ -361,7 +365,7 @@ def tile_localcrossattention_pa_t_kernel(tc, scores, final_encoder_out, WV_w, WV
                 for quarter, o, d_pair in pairs[done["pairs"] : done["pairs"] + PAIRS_PER_STEP]:
                     add_bias_pair(quarter, o, d_pair)
                 done["pairs"] = min(done["pairs"] + PAIRS_PER_STEP, len(pairs))
-            while done["enc_q"] < before["enc"]:
+            while done["enc_q"] < before["enc"] // QUARTER_CHUNKS:
                 quantise_enc(done["enc_q"])
                 done["enc_q"] += 1
             if n >= 6 and n % 2 == 0 and done["attn_q"] < TILES:
@@ -378,7 +382,7 @@ def tile_localcrossattention_pa_t_kernel(tc, scores, final_encoder_out, WV_w, WV
 
         with tc.tile_pool(name="w_prep", bufs=1) as w_prep, tc.tile_pool(
             name="enc_stage", bufs=2 * ENC_PER_STEP
-        ) as enc_stage:
+        ) as enc_stage, tc.tile_pool(name="enc_grp", bufs=2) as enc_grp:
             w_nat = w_prep.tile([P, O * FS // P, FS], BF16)
             nc.sync.dma_start(out=w_nat[:], in_=w_rows)
             load_scores(0)

@@ -315,16 +315,35 @@ def tile_localcrossattention_pa_t_kernel(tc, scores, final_encoder_out, WV_w, WV
             "enc": 0,
             "enc_q": 0,
             "pairs": 0,
+            "biased": 0,
             "v_q": 0,
             "attn_q": 0,
             "attended": 0,
             "picked": 0,
         }
 
+        waiting = []
+
+        def put_pair(n):
+            if n >= FIRST_PAIR_STEP and done["pairs"] < len(pairs):
+                pair = pairs[done["pairs"]]
+                project_pair(*pair)
+                waiting.append(pair)
+                done["pairs"] += 1
+
+        def drain(count):
+            for pair in waiting[:count]:
+                add_bias_pair(*pair)
+                done["biased"] += 1
+            for pair in waiting[:count]:
+                waiting.remove(pair)
+
         def step(n):
             before = dict(done)
+            drain(1)
             if 2 <= n + 1 < HALVES:
                 exp(n + 1)
+            drain(1)
             if n % 2 == 0 and n // 2 + 3 < TILES:
                 load_scores(n // 2 + 3)
             if 0 <= n - 2 < HALVES:
@@ -341,9 +360,7 @@ def tile_localcrossattention_pa_t_kernel(tc, scores, final_encoder_out, WV_w, WV
                 invert(n - 1)
             if 0 <= n - 2 < HALVES:
                 multiply(nc.vector, n - 2, 0, GROUPS - GPSIMD_GROUPS if n - 2 < HALVES - VECTOR_ONLY else GROUPS)
-            if n >= FIRST_PAIR_STEP:
-                for quarter, o, d_pair in pairs[done["pairs"] : done["pairs"] + PAIRS_PER_STEP]:
-                    project_pair(quarter, o, d_pair)
+            put_pair(n)
             for c in range(done["enc"], min(done["enc"] + ENC_PER_STEP, ENC_CHUNKS)):
                 transpose_enc(c)
                 if c + 2 * ENC_PER_STEP < ENC_CHUNKS:
@@ -351,6 +368,7 @@ def tile_localcrossattention_pa_t_kernel(tc, scores, final_encoder_out, WV_w, WV
                 done["enc"] = c + 1
             if 0 <= n - 3 < HALVES:
                 transpose(n - 3)
+            put_pair(n)
             if 0 <= n - 4 < HALVES:
                 g, half = divmod(n - 4, 2)
                 if half == 0:
@@ -361,17 +379,13 @@ def tile_localcrossattention_pa_t_kernel(tc, scores, final_encoder_out, WV_w, WV
             while done["picked"] < before["attended"]:
                 pick_and_store(done["picked"])
                 done["picked"] += 1
-            if n >= FIRST_PAIR_STEP:
-                for quarter, o, d_pair in pairs[done["pairs"] : done["pairs"] + PAIRS_PER_STEP]:
-                    add_bias_pair(quarter, o, d_pair)
-                done["pairs"] = min(done["pairs"] + PAIRS_PER_STEP, len(pairs))
             while done["enc_q"] < before["enc"] // QUARTER_CHUNKS:
                 quantise_enc(done["enc_q"])
                 done["enc_q"] += 1
             if n >= 6 and n % 2 == 0 and done["attn_q"] < TILES:
                 quantise_attn(done["attn_q"])
                 done["attn_q"] += 1
-            while done["v_q"] < before["pairs"] // D_PAIRS:
+            while done["v_q"] < before["biased"] // D_PAIRS:
                 quantise_v(done["v_q"] // O, done["v_q"] % O)
                 done["v_q"] += 1
             for bank in range(OUT_BANKS):

@@ -34,7 +34,9 @@ TILE_BANKS = LQ // BANK_Q
 GPSIMD_GROUPS = 36
 VECTOR_BANK = TILE_BANKS - 1
 
+GPSIMD_GROUPS_LONG = 44
 VECTOR_ONLY = 2
+VECTOR_COPY_TILES = 14
 QUARTERS = 4
 QUARTER_B = B // QUARTERS
 QUARTER_COLS = QUARTER_B * IH
@@ -340,6 +342,10 @@ def tile_localcrossattention_pa_t_kernel(tc, scores, final_encoder_out, WV_w, WV
 
         def step(n):
             before = dict(done)
+            vector_copies = n >= 4 and (n - 4) // 2 < VECTOR_COPY_TILES and (n - 4) % 2 == VECTOR_BANK // HALF_BANKS
+            gpsimd_groups = GPSIMD_GROUPS_LONG if vector_copies else GPSIMD_GROUPS
+            if n - 2 >= HALVES - VECTOR_ONLY:
+                gpsimd_groups = 0
             drain(1)
             if 2 <= n + 1 < HALVES:
                 exp(n + 1)
@@ -348,18 +354,18 @@ def tile_localcrossattention_pa_t_kernel(tc, scores, final_encoder_out, WV_w, WV
                 load_scores(n // 2 + 3)
             if 0 <= n - 2 < HALVES:
                 new_attn(n - 2)
-                if n - 2 < HALVES - VECTOR_ONLY:
-                    multiply(nc.gpsimd, n - 2, GROUPS - GPSIMD_GROUPS, GPSIMD_GROUPS)
+                if gpsimd_groups > 0:
+                    multiply(nc.gpsimd, n - 2, GROUPS - gpsimd_groups, gpsimd_groups)
             if 0 <= n - 1 < HALVES:
                 add_eps(n - 1)
             if n < HALVES:
                 sum_keys(n)
-            if 0 <= n - 4 < HALVES and (n - 4) % 2 == VECTOR_BANK // HALF_BANKS and (n - 4) // 2 < TILES - QUARTER_TILES:
+            if vector_copies:
                 copy_bank(nc.vector.tensor_copy, (n - 4) // 2, VECTOR_BANK)
             if 0 <= n - 1 < HALVES:
                 invert(n - 1)
             if 0 <= n - 2 < HALVES:
-                multiply(nc.vector, n - 2, 0, GROUPS - GPSIMD_GROUPS if n - 2 < HALVES - VECTOR_ONLY else GROUPS)
+                multiply(nc.vector, n - 2, 0, GROUPS - gpsimd_groups)
             put_pair(n)
             for c in range(done["enc"], min(done["enc"] + ENC_PER_STEP, ENC_CHUNKS)):
                 transpose_enc(c)
@@ -374,7 +380,7 @@ def tile_localcrossattention_pa_t_kernel(tc, scores, final_encoder_out, WV_w, WV
                 if half == 0:
                     new_a_grp(g)
                 for bank in range(HALF_BANKS):
-                    if half * HALF_BANKS + bank != VECTOR_BANK or not (g < TILES - QUARTER_TILES):
+                    if half * HALF_BANKS + bank != VECTOR_BANK or g >= VECTOR_COPY_TILES:
                         copy_bank(nc.scalar.copy, g, half * HALF_BANKS + bank)
             while done["picked"] < before["attended"]:
                 pick_and_store(done["picked"])

from contextlib import ExitStack

import concourse.mybir as mybir
from concourse.masks import make_identity

F32 = mybir.dt.float32
BF16 = mybir.dt.bfloat16
U32 = mybir.dt.uint32
U8 = mybir.dt.uint8
I32 = mybir.dt.int32
FP8X4 = mybir.dt.float8_e4m3fn_x4
ACT = mybir.ActivationFunctionType
ALU = mybir.AluOpType

P = 128
PACK = 4
B, O, I, LQ, LS, D = 256, 2, 16, 32, 32, 16
FS = LS * D
EPS = 1e-5
IH = I // PACK
IL = PACK
FLOPS = 2 * (B * I) * FS * (O * FS) + 2 * (B * O) * LQ * (I * LS) * D

ROW = IL * LQ * LS
TILES = B * O * IH // P
TILE_B = P // (O * IH)
HALVES = 2 * TILES
HALF_Q = LQ // 2
GROUPS = HALF_Q * IL
HALF = GROUPS * LS
BANK_Q = 8
HALF_BANKS = HALF_Q // BANK_Q
TILE_BANKS = LQ // BANK_Q
GPSIMD_GROUPS = 36
VECTOR_BANK = TILE_BANKS - 1

GPSIMD_GROUPS_LONG = 44
VECTOR_ONLY = 2
VECTOR_COPY_TILES = 14
QUARTERS = 4
QUARTER_B = B // QUARTERS
QUARTER_COLS = QUARTER_B * IH
QUARTER_TILES = TILES // QUARTERS
ENC_CHUNKS = B * IH // P
QUARTER_CHUNKS = ENC_CHUNKS // QUARTERS
GROUP_B = 4
TILE_GROUPS = TILE_B // GROUP_B
PASS_COLS = D * GROUP_B
V_COLS = QUARTER_B * D
ZERO_COLS = P - LS
D_PAIRS = D // 2
OUT_BANKS = 2

PAIRS_PER_STEP = 2
FIRST_PAIR_STEP = 2
ENC_PER_STEP = 2
WARMUP_STEPS = ENC_CHUNKS // ENC_PER_STEP + 1


def tile_localcrossattention_pa_t_kernel(tc, scores, final_encoder_out, WV_w, WV_b, out):
    nc = tc.nc

    score_rows = scores.rearrange("b o (h l) q k -> (b o h) (l q k)", h=IH)
    enc_rows = final_encoder_out.rearrange("b (h l s) d -> (b h) (l s d)", h=IH, l=IL)
    w_rows = WV_w.rearrange("o (c p) f -> p (o c) f", p=P)
    out_view = out.rearrange("(n j) (o q) d -> j o q n d", j=GROUP_B, o=O)

    with ExitStack() as stack:
        stack.enter_context(tc.manual_schedule())
        const = stack.enter_context(tc.tile_pool(name="const", bufs=1))
        x_pool = stack.enter_context(tc.tile_pool(name="x", bufs=3))
        e_pool = stack.enter_context(tc.tile_pool(name="e", bufs=5))
        sum_pool = stack.enter_context(tc.tile_pool(name="sums", bufs=4))
        attn_pool = stack.enter_context(tc.tile_pool(name="attn", bufs=3))
        a_stage = stack.enter_context(tc.tile_pool(name="a_stage", bufs=2))
        v_stage = stack.enter_context(tc.tile_pool(name="v_stage", bufs=2))
        v_keep = stack.enter_context(tc.tile_pool(name="v_keep", bufs=4))
        ps_t = stack.enter_context(tc.psum_pool(name="ps_t", bufs=4))
        ps_v = stack.enter_context(tc.psum_pool(name="ps_v", bufs=2))
        ps_out = stack.enter_context(tc.psum_pool(name="ps_out", bufs=OUT_BANKS))

        ident_f32 = const.tile([P, P], F32)
        make_identity(nc, ident_f32[:])
        ident_bf = const.tile([P, P], BF16)
        make_identity(nc, ident_bf[:])

        z_codes = const.tile([P, O * D * P + ZERO_COLS], U32, align_bytes=64)
        nc.vector.memset(z_codes[:].bitcast(I32), 0)
        z_scales = const.tile([P, O * D * P], U8, align_bytes=64)
        enc_codes = const.tile([P, QUARTERS, IL, QUARTER_COLS], U32, align_bytes=64)
        enc_scales = const.tile([P, QUARTERS, IL, QUARTER_COLS], U8, align_bytes=64)
        bias_bf = const.tile([P, O * D], BF16)
        bias_col = const.tile([P, O * D], F32)

        x_tiles = {}
        e_tiles = {}

        def load_scores(g):
            x = x_pool.tile([P, ROW], BF16, name="x", tag="x")
            nc.sync.dma_start(out=x[:], in_=score_rows[g * P : (g + 1) * P, :])
            x_tiles[g] = x

        def exp(h):
            g, half = divmod(h, 2)
            x_by_query = x_tiles[g][:].rearrange("p (l q k) -> p q l k", l=IL, q=LQ)
            e = e_pool.tile([P, HALF], F32, name="e", tag="e")
            nc.scalar.activation(
                out=e[:].rearrange("p (q l k) -> p q l k", l=IL, k=LS),
                in_=x_by_query[:, half * HALF_Q : (half + 1) * HALF_Q],
                func=ACT.Exp,
            )
            e_tiles[h] = e

        sums_of = {}
        denom_of = {}
        recip_of = {}
        attn_of = {}

        def sum_keys(h):
            sums = sum_pool.tile([P, GROUPS], F32, name="sums", tag="sums")
            nc.vector.tensor_reduce(
                out=sums[:],
                in_=e_tiles[h][:].rearrange("p (g k) -> p g k", k=LS),
                axis=mybir.AxisListType.X,
                op=ALU.add,
            )
            sums_of[h] = sums

        def add_eps(h):
            denom = sum_pool.tile([P, GROUPS], F32, name="denom", tag="denom")
            nc.vector.tensor_scalar_add(out=denom[:], in0=sums_of[h][:], scalar1=EPS)
            denom_of[h] = denom

        def invert(h):
            recip = sum_pool.tile([P, GROUPS], F32, name="recip", tag="recip")
            nc.vector.reciprocal(out=recip[:], in_=denom_of[h][:])
            recip_of[h] = recip

        def new_attn(h):
            attn = attn_pool.tile([P, HALF], BF16, name="attn", tag="attn")
            attn_of[h] = attn

        def multiply(engine, h, first, count):
            groups = slice(first, first + count)
            engine.tensor_tensor(
                out=attn_of[h][:].rearrange("p (g k) -> p g k", k=LS)[:, groups, :],
                in0=e_tiles[h][:].rearrange("p (g k) -> p g k", k=LS)[:, groups, :],
                in1=recip_of[h][:, groups].unsqueeze(2).to_broadcast([P, count, LS]),
                op=ALU.mult,
            )

        banks_of = {}
        a_grp_of = {}
        attn_q = {}

        def transpose(h):
            banks_of[h] = []
            for bank in range(HALF_BANKS):
                at = ps_t.tile([P, O * TILE_B * BANK_Q * PACK], BF16, name="at", tag="t")
                at_by_query = at[:].rearrange("p (o b q t) -> p b o q t", o=O, b=TILE_B, q=BANK_Q)
                for qi in range(BANK_Q):
                    q = bank * BANK_Q + qi
                    nc.tensor.transpose(
                        out=at_by_query[:, :, :, qi, :],
                        in_=attn_of[h][:, q * P : (q + 1) * P],
                        identity=ident_bf[:],
                    )
                banks_of[h].append(at)

        def new_a_grp(g):
            a_grp_of[g] = a_stage.tile([P, ROW], BF16, name="a_grp", tag="a_grp", align_bytes=64)

        def copy_bank(copy, g, tile_bank):
            half, bank = divmod(tile_bank, HALF_BANKS)
            a_grp_banks = a_grp_of[g][:].rearrange(
                "p (c n x) -> p c n x", n=TILE_BANKS, x=BANK_Q * PACK
            )
            copy(
                out=a_grp_banks[:, :, tile_bank, :],
                in_=banks_of[2 * g + half][bank][:].rearrange("p (c x) -> p c x", x=BANK_Q * PACK),
            )

        def quantise_attn(g):
            a_codes = a_keep.tile([P, ROW // PACK], U32, name="a_codes", tag="a_codes", align_bytes=64)
            a_scales = a_keep.tile([P, ROW // PACK], U8, name="a_scales", tag="a_scales", align_bytes=64)
            nc.vector.quantize_mx(out=a_codes[:].bitcast(FP8X4), scales=a_scales[:], in_=a_grp_of[g][:])
            attn_q[g] = (a_codes, a_scales)

        v_grp_of = {}
        v_q = {}

        acc_of = {}

        def project_pair(quarter, o, d_pair):
            acc = ps_v.tile([P, 2, QUARTER_COLS], F32, name="acc", tag="acc")
            for di in range(2):
                od = o * D + 2 * d_pair + di
                for il in range(IL):
                    first = od * P + ZERO_COLS - il * LS
                    nc.tensor.matmul_mx(
                        out=acc[:, di, :],
                        lhsT=z_codes[:, first : first + P].bitcast(FP8X4),
                        lhsT_scale=z_scales[:, od * P : (od + 1) * P],
                        rhs=enc_codes[:, quarter, il].bitcast(FP8X4),
                        rhs_scale=enc_scales[:, quarter, il],
                        start=(il == 0),
                        stop=(il == IL - 1),
                    )
            acc_of[(quarter, o, d_pair)] = acc

        def add_bias_pair(quarter, o, d_pair):
            if d_pair == 0:
                v_grp_of[(quarter, o)] = v_stage.tile(
                    [P, V_COLS * PACK], BF16, name="v_grp", tag="v_grp", align_bytes=64
                )
            v_grp_by_d = v_grp_of[(quarter, o)][:].rearrange("p (n d x) -> p n d x", d=D, x=GROUP_B * PACK)
            for di in range(2):
                d = 2 * d_pair + di
                nc.scalar.activation(
                    out=v_grp_by_d[:, :, d, :],
                    in_=acc_of[(quarter, o, d_pair)][:, di, :].rearrange("p (n x) -> p n x", x=GROUP_B * PACK),
                    func=ACT.Identity,
                    bias=bias_col[:, o * D + d : o * D + d + 1],
                )

        def quantise_v(quarter, o):
            v_codes = v_keep.tile([P, V_COLS], U32, name="v_codes", tag="v_codes", align_bytes=64)
            v_scales = v_keep.tile([P, V_COLS], U8, name="v_scales", tag="v_scales", align_bytes=64)
            nc.vector.quantize_mx(
                out=v_codes[:].bitcast(FP8X4), scales=v_scales[:], in_=v_grp_of[(quarter, o)][:]
            )
            v_q[(quarter, o)] = (v_codes, v_scales)

        o_acc_of = {}
        res_of = {}

        def attend(g):
            quarter, gi = divmod(g, QUARTER_TILES)
            a_codes, a_scales = attn_q[g]
            o_acc = ps_out.tile([P, O, TILE_GROUPS, D, GROUP_B], F32, name="o_acc", tag="o_acc")
            for o in range(O):
                v_codes, v_scales = v_q[(quarter, o)]
                for s in range(TILE_GROUPS):
                    a_cols = slice((o * TILE_GROUPS + s) * P, (o * TILE_GROUPS + s + 1) * P)
                    v_cols = slice((gi * TILE_GROUPS + s) * PASS_COLS, (gi * TILE_GROUPS + s + 1) * PASS_COLS)
                    nc.tensor.matmul_mx(
                        out=o_acc[:, o, s].rearrange("p d j -> p (d j)"),
                        lhsT=a_codes[:, a_cols].bitcast(FP8X4),
                        lhsT_scale=a_scales[:, a_cols],
                        rhs=v_codes[:, v_cols].bitcast(FP8X4),
                        rhs_scale=v_scales[:, v_cols],
                        start=True,
                        stop=True,
                    )
            o_acc_of[g] = o_acc

        def pick_and_store(g):
            quarter, gi = divmod(g, QUARTER_TILES)
            if gi == 0:
                res_of[quarter] = res_pool.tile(
                    [P, O, QUARTER_TILES, TILE_GROUPS, GROUP_B, D], F32, name="res", tag="res"
                )
            res = res_of[quarter]
            nc.scalar.mul(
                out=res[:, :, gi],
                in_=o_acc_of[g][:].rearrange("p o s d j -> p o s j d"),
                mul=1.0 / 4.0,
            )
            if gi == QUARTER_TILES - 1:
                n_groups = QUARTER_TILES * TILE_GROUPS
                for j in range(GROUP_B):
                    for o in range(O):
                        nc.sync.dma_start(
                            out=out_view[j, o, :, quarter * n_groups : (quarter + 1) * n_groups, :],
                            in_=res[j * LQ : (j + 1) * LQ, o, :, :, j, :].rearrange("q g s d -> q (g s) d"),
                        )

        e_nat_of = {}
        e_grp_of = {}

        def load_enc(c):
            e_nat = enc_stage.tile([P, IL * FS], BF16, name="e_nat", tag="e_nat")
            nc.sync.dma_start(out=e_nat[:], in_=enc_rows[c * P : (c + 1) * P, :])
            e_nat_of[c] = e_nat

        def transpose_enc(c):
            e_words = e_nat_of[c][:].bitcast(F32)
            quarter, part = divmod(c, QUARTER_CHUNKS)
            if part == 0:
                e_grp_of[quarter] = enc_grp.tile(
                    [P, IL * QUARTER_COLS * PACK], BF16, name="e_grp", tag="e_grp", align_bytes=64
                )
            e_grp_words = e_grp_of[quarter][:].bitcast(F32).rearrange("p (l m u) -> p l m u", l=IL, u=2)
            rows = slice(part * P, (part + 1) * P)
            for pair in range(IL // 2):
                et = ps_t.tile([P, 2, 2, P], F32, name="et", tag="t")
                for li in range(2):
                    for u in range(2):
                        first = ((2 * pair + li) * 2 + u) * P
                        nc.tensor.transpose(
                            out=et[:, li, u, :], in_=e_words[:, first : first + P], identity=ident_f32[:]
                        )
                nc.scalar.copy(
                    out=e_grp_words[:, 2 * pair : 2 * pair + 2, rows, :],
                    in_=et[:].rearrange("p l u m -> p l m u"),
                )

        def quantise_enc(quarter):
            nc.vector.quantize_mx(
                out=enc_codes[:, quarter].rearrange("p l m -> p (l m)").bitcast(FP8X4),
                scales=enc_scales[:, quarter].rearrange("p l m -> p (l m)"),
                in_=e_grp_of[quarter][:],
            )

        pairs = [(quarter, o, d_pair) for quarter in range(QUARTERS) for o in range(O) for d_pair in range(D_PAIRS)]
        done = {
            "enc": 0,
            "enc_q": 0,
            "pairs": 0,
            "biased": 0,
            "v_q": 0,
            "attn_q": 0,
            "attended": 0,
            "picked": 0,
        }

        waiting = []

        def put_pair(n):
            if n >= FIRST_PAIR_STEP and done["pairs"] < len(pairs):
                pair = pairs[done["pairs"]]
                project_pair(*pair)
                waiting.append(pair)
                done["pairs"] += 1

        def drain(count):
            for pair in waiting[:count]:
                add_bias_pair(*pair)
                done["biased"] += 1
            for pair in waiting[:count]:
                waiting.remove(pair)

        def step(n):
            before = dict(done)
            vector_copies = n >= 4 and (n - 4) // 2 < VECTOR_COPY_TILES and (n - 4) % 2 == VECTOR_BANK // HALF_BANKS
            gpsimd_groups = GPSIMD_GROUPS_LONG if vector_copies else GPSIMD_GROUPS
            if n - 2 >= HALVES - VECTOR_ONLY:
                gpsimd_groups = 0
            drain(1)
            if 2 <= n + 1 < HALVES:
                exp(n + 1)
            drain(1)
            if n % 2 == 0 and n // 2 + 3 < TILES:
                load_scores(n // 2 + 3)
            if 0 <= n - 2 < HALVES:
                new_attn(n - 2)
                if gpsimd_groups > 0:
                    multiply(nc.gpsimd, n - 2, GROUPS - gpsimd_groups, gpsimd_groups)
            if 0 <= n - 1 < HALVES:
                add_eps(n - 1)
            if n < HALVES:
                sum_keys(n)
            if vector_copies:
                copy_bank(nc.vector.tensor_copy, (n - 4) // 2, VECTOR_BANK)
            if 0 <= n - 1 < HALVES:
                invert(n - 1)
            if 0 <= n - 2 < HALVES:
                multiply(nc.vector, n - 2, 0, GROUPS - gpsimd_groups)
            put_pair(n)
            for c in range(done["enc"], min(done["enc"] + ENC_PER_STEP, ENC_CHUNKS)):
                transpose_enc(c)
                if c + 2 * ENC_PER_STEP < ENC_CHUNKS:
                    load_enc(c + 2 * ENC_PER_STEP)
                done["enc"] = c + 1
            if 0 <= n - 3 < HALVES:
                transpose(n - 3)
            put_pair(n)
            if 0 <= n - 4 < HALVES:
                g, half = divmod(n - 4, 2)
                if half == 0:
                    new_a_grp(g)
                for bank in range(HALF_BANKS):
                    if half * HALF_BANKS + bank != VECTOR_BANK or g >= VECTOR_COPY_TILES:
                        copy_bank(nc.scalar.copy, g, half * HALF_BANKS + bank)
            while done["picked"] < before["attended"]:
                pick_and_store(done["picked"])
                done["picked"] += 1
            while done["enc_q"] < before["enc"] // QUARTER_CHUNKS:
                quantise_enc(done["enc_q"])
                done["enc_q"] += 1
            if n >= 6 and n % 2 == 0 and done["attn_q"] < TILES:
                quantise_attn(done["attn_q"])
                done["attn_q"] += 1
            while done["v_q"] < before["biased"] // D_PAIRS:
                quantise_v(done["v_q"] // O, done["v_q"] % O)
                done["v_q"] += 1
            for bank in range(OUT_BANKS):
                g = done["attended"]
                if g < before["attn_q"] and O * (g // QUARTER_TILES + 1) <= before["v_q"]:
                    attend(g)
                    done["attended"] += 1

        with tc.tile_pool(name="w_prep", bufs=1) as w_prep, tc.tile_pool(
            name="enc_stage", bufs=2 * ENC_PER_STEP
        ) as enc_stage, tc.tile_pool(name="enc_grp", bufs=2) as enc_grp:
            w_nat = w_prep.tile([P, O * FS // P, FS], BF16)
            nc.sync.dma_start(out=w_nat[:], in_=w_rows)
            load_scores(0)
            for il in range(IL):
                nc.sync.dma_start(
                    out=bias_bf[il * LS : (il + 1) * LS, :].rearrange("k (o d) -> k o d", o=O),
                    in_=WV_b.rearrange("o (k d) -> k o d", d=D),
                )
            load_enc(0)
            load_enc(1)
            load_scores(1)
            load_enc(2)
            load_enc(3)
            load_scores(2)
            exp(0)
            exp(1)

            w_scales = w_prep.tile([P, O * FS], U8, align_bytes=64)
            nc.vector.memset(w_scales[:].bitcast(I32), 0)
            w_grp = w_prep.tile([P, O * FS * PACK], BF16, align_bytes=64)
            w_grp_words = w_grp[:].bitcast(F32).rearrange("p (o d k u) -> p o d k u", o=O, d=D, k=LS)
            k_rows = P // D
            for pair in range(O * FS // P // 2):
                wt = ps_t.tile([P, 2, 2, P], F32, name="wt", tag="t")
                for ci in range(2):
                    w_words = w_nat[:, 2 * pair + ci, :].bitcast(F32)
                    for u in range(2):
                        nc.tensor.transpose(
                            out=wt[:, ci, u, :], in_=w_words[:, u * P : (u + 1) * P], identity=ident_f32[:]
                        )
                for ci in range(2):
                    o, kc = divmod(2 * pair + ci, LS // k_rows)
                    nc.vector.tensor_copy(
                        out=w_grp_words[:, o, :, kc * k_rows : (kc + 1) * k_rows, :],
                        in_=wt[:, ci].rearrange("p u (k d) -> p d k u", d=D),
                    )
            nc.vector.tensor_copy(out=bias_col[:], in_=bias_bf[:])
            w_codes = w_prep.tile([P, O * FS], U32, align_bytes=64)
            nc.vector.quantize_mx(out=w_codes[:].bitcast(FP8X4), scales=w_scales[:], in_=w_grp[:])

            step(0)
            nc.vector.tensor_copy(
                out=z_codes[:, 0 : O * D * P].bitcast(I32).rearrange("p (g c) -> p g c", c=P)[:, :, ZERO_COLS:P],
                in_=w_codes[:].bitcast(I32).rearrange("p (g k) -> p g k", k=LS),
            )
            z_scale_words = z_scales[:].bitcast(I32).rearrange("p (g r w) -> p g r w", r=IL, w=LS // 4)
            for il in range(IL):
                nc.vector.tensor_copy(
                    out=z_scale_words[:, :, il, :],
                    in_=w_scales[:].bitcast(I32).rearrange("p (g w) -> p g w", w=LS // 4),
                )
            for n in range(1, WARMUP_STEPS):
                step(n)

        a_keep = stack.enter_context(tc.tile_pool(name="a_keep", bufs=4))
        res_pool = stack.enter_context(tc.tile_pool(name="res", bufs=2))
        n = WARMUP_STEPS
        while done["picked"] < TILES:
            step(n)
            n += 1
